import numpy as np
import ml_dtypes


def mxq(x, axis, fmt="e4m3"):
    dtype, down = {"e4m3": (ml_dtypes.float8_e4m3fn, 7), "e5m2": (ml_dtypes.float8_e5m2, 14)}[fmt]
    v = np.moveaxis(np.asarray(x, np.float32).astype(ml_dtypes.bfloat16).astype(np.float64), axis, -1)
    blocks = v.reshape(v.shape[:-1] + (-1, 32))
    amax = np.abs(blocks).max(-1, keepdims=True)
    byte = np.maximum(np.where(amax > 0, np.frexp(amax)[1] - 1 + 127, 0) - down, 1)
    scale = np.exp2(byte - 127.0)
    codes = (blocks / scale).astype(np.float32).astype(dtype).astype(np.float64)
    return np.moveaxis((codes * scale).reshape(v.shape), -1, axis)


WIDE = False


def mx_kscale(k):
    if not WIDE:
        return np.ones(k)
    levels = np.array([10, -10, 5, -5, 0])
    a = np.random.permutation(np.resize(levels, k // 512 * 4)).reshape(k // 512, 4)
    idx = np.arange(k)
    return np.exp2(a[idx // 512, idx % 128 // 32])


BF16 = ml_dtypes.bfloat16


def bf(x):
    return np.asarray(x, np.float32).astype(BF16)


def f64(x):
    return np.asarray(x).astype(np.float64)


B, C, H, W, HS, WS = 4, 512, 32, 32, 16, 32
N = H * W
EPS = 1e-5


def mean_variance_norm(flat):
    mu = flat.mean(axis=-1, keepdims=True)
    sd = np.sqrt(flat.var(axis=-1, ddof=1, keepdims=True) + EPS)
    return (flat - mu) / sd


def setup_inputs():
    s = mx_kscale(C)
    gain = 0.7 + 0.6 * np.random.random_sample((B, C, 1, 1))
    shift = 0.4 * np.random.standard_normal((B, C, 1, 1))
    return {"content": bf(np.random.standard_normal((B, C, H, W)) * gain + shift),
            "mean": bf(np.random.standard_normal((B, C, H, W)) * 0.3 * s[:, None, None]),
            "std": bf(np.abs(1.0 + 0.25 * np.random.standard_normal((B, C, H, W))) * s[:, None, None]),
            "out_w": bf(np.random.standard_normal((C, C)) / np.sqrt(C) / s),
            "out_b": bf(np.random.standard_normal(C) * 0.2)}


def reference(content, mean, std, out_w, out_b):
    x = f64(content).reshape(B, C, N)
    o = f64(std).reshape(B, C, N) * mean_variance_norm(x) + f64(mean).reshape(B, C, N)
    y = (mxq(f64(out_w), 1, "e4m3") @ mxq(o, 1, "e4m3")) + f64(out_b)[:, None]
    return (y + x).reshape(B, C, H, W)

@@ -1,0 +1,282 @@
+from contextlib import ExitStack
+
+import concourse.mybir as mybir
+from concourse.masks import make_identity
+
+F32 = mybir.dt.float32
+BF16 = mybir.dt.bfloat16
+U32 = mybir.dt.uint32
+U8 = mybir.dt.uint8
+FP8X4 = mybir.dt.float8_e4m3fn_x4
+ALU = mybir.AluOpType
+ACT = mybir.ActivationFunctionType
+
+B = 4
+C = 512
+NPIX = 1024
+P = 128
+J = 4
+HALF = 512
+UNITS = 2 * B
+EPS = 1e-5
+FLOPS = 2 * C * C * B * NPIX
+
+VJ = {0: [0, 2, 3], 1: [0, 1], 2: [], 3: []}
+GJ = [0, 0, 0, 0, 0, 0, 0, 0]
+RUN = 4
+
+
+def tile_aattn_pb_t_kernel(tc, content, mean, std, out_w, out_b, out):
+    nc = tc.nc
+    xv = content.rearrange("b (p j) h w -> b p j (h w)", j=J)
+    mv_ = mean.rearrange("b (p j) h w -> b p j (h w)", j=J)
+    sv = std.rearrange("b (p j) h w -> b p j (h w)", j=J)
+    ov = out.rearrange("b (p j) h w -> b p j (h w)", j=J)
+    wv = out_w.rearrange("(m j) c -> m j c", j=J)
+    bv = out_b.rearrange("(p j) -> p j", j=J)
+
+    with ExitStack() as ctx:
+        keep = ctx.enter_context(tc.tile_pool(name="keep", bufs=1))
+        nmp = ctx.enter_context(tc.tile_pool(name="nmp", bufs=4))
+        mp = ctx.enter_context(tc.tile_pool(name="mp", bufs=1))
+        ogp = ctx.enter_context(tc.tile_pool(name="ogp", bufs=2))
+        cdp = ctx.enter_context(tc.tile_pool(name="cdp", bufs=2))
+        otp = ctx.enter_context(tc.tile_pool(name="otp", bufs=4))
+        psum = ctx.enter_context(tc.psum_pool(name="psum", bufs=8))
+        ctx.enter_context(tc.manual_schedule())
+
+        eps_t = keep.tile([P, 1], F32, name="eps_t")
+        one_t = keep.tile([P, 1], F32, name="one_t")
+        warm_t = keep.tile([P, 1], F32, name="warm_t")
+        nc.vector.memset(one_t[:], 1.0)
+        nc.vector.memset(eps_t[:], EPS)
+        nc.scalar.activation(out=warm_t[:], in_=one_t[:], func=ACT.Sqrt)
+        ident = keep.tile([P, P], F32, name="ident")
+        make_identity(nc, ident[:])
+
+        x_t = [keep.tile([P, J, NPIX], BF16, name="x%d" % b) for b in range(B)]
+        s_t = [keep.tile([P, J, NPIX], BF16, name="s%d" % b) for b in range(B)]
+        m_t = [keep.tile([P, J, NPIX], BF16, name="m%d" % b) for b in range(B)]
+        w_sb = keep.tile([P, J, C], BF16, name="w_sb")
+        b_bf = keep.tile([P, J], BF16, name="b_bf")
+        for j in range(J):
+            nc.sync.dma_start(out=x_t[0][:, j, :], in_=xv[0][:, j, :])
+        nc.sync.dma_start(out=s_t[0][:], in_=sv[0])
+        nc.sync.dma_start(out=m_t[0][:], in_=mv_[0])
+        nc.sync.dma_start(out=w_sb[:], in_=wv)
+        nc.sync.dma_start(out=x_t[1][:, 0:2, :], in_=xv[1][:, 0:2, :])
+        nc.sync.dma_start(out=x_t[1][:, 2:4, :], in_=xv[1][:, 2:4, :])
+        nc.sync.dma_start(out=b_bf[:], in_=bv)
+        nc.sync.dma_start(out=s_t[1][:], in_=sv[1])
+        nc.sync.dma_start(out=m_t[1][:], in_=mv_[1])
+        for b in range(2, B):
+            nc.sync.dma_start(out=x_t[b][:], in_=xv[b])
+            nc.sync.dma_start(out=s_t[b][:], in_=sv[b])
+            nc.sync.dma_start(out=m_t[b][:], in_=mv_[b])
+
+        junkp = ctx.enter_context(tc.tile_pool(name="junkp", bufs=4))
+        b_f = keep.tile([P, J], F32, name="b_f")
+
+        rstd_ap = {}
+        nbias_ap = {}
+        st8 = {}
+
+        def stats_scalar(b):
+            js = [j for j in range(J) if j not in VJ[b]]
+            if not js:
+                return
+            n = len(js)
+            sm = keep.tile([P, n], F32, name="sm%d" % b)
+            ng = keep.tile([P, n], F32, name="ng%d" % b)
+            sq = keep.tile([P, n], F32, name="sq%d" % b)
+            sd = keep.tile([P, n], F32, name="sds%d" % b)
+            for k, j in enumerate(js):
+                junk = junkp.tile([P, NPIX], BF16, name="junk")
+                nc.scalar.activation(out=junk[:], in_=x_t[b][:, j, :], func=ACT.Identity,
+                                     accum_out=sm[:, k:k + 1])
+            nc.scalar.mul(out=ng[:], in_=sm[:], mul=-1.0 / NPIX)
+            for k, j in enumerate(js):
+                junk = junkp.tile([P, NPIX], BF16, name="junk")
+                nc.scalar.activation(out=junk[:], in_=x_t[b][:, j, :], func=ACT.Square,
+                                     bias=ng[:, k:k + 1], accum_out=sq[:, k:k + 1])
+            nc.scalar.activation(out=sd[:], in_=sq[:], func=ACT.Sqrt,
+                                 scale=1.0 / (NPIX - 1), bias=eps_t[:, 0:1])
+            st8[("s", b)] = (js, ng, sd)
+
+        def stats_vector(b):
+            js = VJ[b]
+            if not js:
+                return
+            n = len(js)
+            st = keep.tile([P, n, 2, 6], F32, name="st%d" % b)
+            ag = keep.tile([P, n, 2], F32, name="ag%d" % b)
+            vv = keep.tile([P, n], F32, name="vv%d" % b)
+            for k, j in enumerate(js):
+                for c in range(2):
+                    nc.vector.bn_stats(out=st[:, k, c, :], in_=x_t[b][:, j, c * HALF:(c + 1) * HALF])
+                if k > 0:
+                    nc.vector.bn_aggr(out=ag[:, k - 1, :], in_=st[:, k - 1, :, :].rearrange("p c s -> p (c s)"))
+            nc.vector.bn_aggr(out=ag[:, n - 1, :], in_=st[:, n - 1, :, :].rearrange("p c s -> p (c s)"))
+            nc.vector.tensor_scalar(out=vv[:], in0=ag[:, :, 1], scalar1=float(NPIX) / (NPIX - 1),
+                                    scalar2=EPS, op0=ALU.mult, op1=ALU.add)
+            st8[("v", b)] = (js, ag, vv)
+
+        def sqrt_vector_group(b):
+            if ("v", b) not in st8:
+                return
+            js, ag, vv = st8[("v", b)]
+            sd = keep.tile([P, len(js)], F32, name="sdv%d" % b)
+            nc.scalar.activation(out=sd[:], in_=vv[:], func=ACT.Sqrt)
+            st8[("v2", b)] = sd
+
+        def chain(b):
+            if ("v", b) in st8:
+                js, ag, vv = st8[("v", b)]
+                sd = st8[("v2", b)]
+                rs = keep.tile([P, len(js)], F32, name="rsv%d" % b)
+                nb = keep.tile([P, len(js)], F32, name="nbv%d" % b)
+                nc.vector.reciprocal(out=rs[:], in_=sd[:])
+                nc.vector.scalar_tensor_tensor(out=nb[:], in0=ag[:, :, 0], scalar=-1.0, in1=rs[:],
+                                               op0=ALU.mult, op1=ALU.mult)
+                for k, j in enumerate(js):
+                    rstd_ap[(b, j)] = rs[:, k:k + 1]
+                    nbias_ap[(b, j)] = nb[:, k:k + 1]
+            if ("s", b) in st8:
+                js, ng, sd = st8[("s", b)]
+                rs = keep.tile([P, len(js)], F32, name="rss%d" % b)
+                nb = keep.tile([P, len(js)], F32, name="nbs%d" % b)
+                nc.vector.reciprocal(out=rs[:], in_=sd[:])
+                nc.vector.tensor_tensor(out=nb[:], in0=ng[:], in1=rs[:], op=ALU.mult)
+                for k, j in enumerate(js):
+                    rstd_ap[(b, j)] = rs[:, k:k + 1]
+                    nbias_ap[(b, j)] = nb[:, k:k + 1]
+
+        nm_u = {}
+        pr_u = {}
+        og_u = {}
+        cd_u = {}
+        ac_u = {}
+
+        def cols(u):
+            h = u % 2
+            return slice(h * HALF, (h + 1) * HALF)
+
+        def norm(u):
+            b = u // 2
+            nm = nmp.tile([P, J, HALF], F32, name="nm")
+            nm_u[u] = nm
+            for j in range(J):
+                nc.scalar.activation(out=nm[:, j, :], in_=x_t[b][:, j, cols(u)], func=ACT.Identity,
+                                     scale=rstd_ap[(b, j)], bias=nbias_ap[(b, j)])
+
+        def prod_gpsimd(u):
+            b = u // 2
+            pr = mp.tile([P, J, HALF], F32, name="pr")
+            pr_u[u] = pr
+            g = GJ[u]
+            if g:
+                nc.gpsimd.tensor_tensor(out=pr[:, J - g:J, :], in0=nm_u[u][:, J - g:J, :],
+                                        in1=s_t[b][:, J - g:J, cols(u)], op=ALU.mult)
+
+        def prod_vector(u, split=False):
+            b = u // 2
+            pr = pr_u[u]
+            v = J - GJ[u]
+            if split:
+                for j in range(v):
+                    nc.vector.tensor_tensor(out=pr[:, j, :], in0=nm_u[u][:, j, :],
+                                            in1=s_t[b][:, j, cols(u)], op=ALU.mult)
+            else:
+                nc.vector.tensor_tensor(out=pr[:, 0:v, :], in0=nm_u[u][:, 0:v, :],
+                                        in1=s_t[b][:, 0:v, cols(u)], op=ALU.mult)
+
+        def add_regroup(u):
+            b = u // 2
+            og = ogp.tile([P, HALF * J], BF16, name="og", align_bytes=64)
+            og_u[u] = og
+            nc.vector.tensor_tensor(
+                out=og[:].rearrange("p (c i t) -> p c t i", i=RUN, t=J),
+                in0=pr_u[u][:].rearrange("p t (c i) -> p c t i", i=RUN),
+                in1=m_t[b][:, :, cols(u)].rearrange("p t (c i) -> p c t i", i=RUN),
+                op=ALU.add)
+
+        def quantise(u):
+            cd = cdp.tile([P, HALF], U32, name="cd", align_bytes=64)
+            sc = cdp.tile([P, HALF], U8, name="sc", align_bytes=64)
+            cd_u[u] = (cd, sc)
+            nc.vector.quantize_mx(out=cd[:].bitcast(FP8X4), scales=sc[:], in_=og_u[u][:])
+
+        def multiply(u):
+            cd, sc = cd_u[u]
+            accs = []
+            for j in range(J):
+                acc = psum.tile([P, HALF], F32, name="acc", tag="bank")
+                nc.tensor.matmul_mx(out=acc[:], lhsT=w_cd[:, j * P:(j + 1) * P].bitcast(FP8X4),
+                                    lhsT_scale=w_sc[:, j * P:(j + 1) * P],
+                                    rhs=cd[:].bitcast(FP8X4), rhs_scale=sc[:],
+                                    start=True, stop=True)
+                accs.append(acc)
+            ac_u[u] = accs
+
+        def finish(u):
+            b = u // 2
+            ot = otp.tile([P, J, HALF], F32, name="ot")
+            for j in range(J):
+                nc.vector.scalar_tensor_tensor(out=ot[:, j, :], in0=ac_u[u][j][:], scalar=b_f[:, j:j + 1],
+                                               in1=x_t[b][:, j, cols(u)], op0=ALU.add, op1=ALU.add)
+            nc.sync.dma_start(out=ov[b][:, :, cols(u)], in_=ot[:])
+
+        w_g = keep.tile([P, C * J], BF16, name="w_g", align_bytes=64)
+        w_cd = keep.tile([P, C], U32, name="w_cd", align_bytes=64)
+        w_sc = keep.tile([P, C], U8, name="w_sc", align_bytes=64)
+
+        def weights_transpose():
+            w32 = w_sb[:].bitcast(F32).rearrange("p j (q u) -> p j q u", u=2)
+            g32 = w_g[:].bitcast(F32)
+            for hh in range(2):
+                wt = psum.tile([P, 2, 2, P], F32, name="wt", tag="bank")
+                for a in range(2):
+                    for u2 in range(2):
+                        nc.tensor.transpose(wt[:, a, u2, :], w32[:, 2 * hh + a, :, u2], ident[:])
+                nc.scalar.copy(out=g32[:, hh * 512:(hh + 1) * 512].rearrange("p (a m u) -> p a m u", a=2, u=2),
+                               in_=wt[:].rearrange("p a u m -> p a m u"))
+
+        def weights_quantise():
+            nc.vector.quantize_mx(out=w_cd[:].bitcast(FP8X4), scales=w_sc[:], in_=w_g[:])
+
+        stats_scalar(0)
+        stats_vector(0)
+        sqrt_vector_group(0)
+        chain(0)
+        norm(0)
+        prod_gpsimd(0)
+        prod_vector(0, split=True)
+        norm(1)
+        weights_transpose()
+        add_regroup(0)
+        nc.vector.tensor_copy(out=b_f[:], in_=b_bf[:])
+        stats_vector(1)
+        stats_scalar(1)
+        sqrt_vector_group(1)
+        for u in range(UNITS):
+            nxt = u + 1
+            if nxt < UNITS:
+                if nxt not in pr_u:
+                    prod_gpsimd(nxt)
+                prod_vector(nxt)
+            if u == 0:
+                weights_quantise()
+            quantise(u)
+            multiply(u)
+            if u % 2 == 0 and u // 2 + 1 < B:
+                b = u // 2 + 1
+                chain(b)
+                norm(2 * b)
+                norm(2 * b + 1)
+                if b + 1 < B:
+                    stats_vector(b + 1)
+                    stats_scalar(b + 1)
+                    sqrt_vector_group(b + 1)
+            if nxt < UNITS:
+                add_regroup(nxt)
+            finish(u)

@@ -21,15 +21,19 @@ UNITS = 2 * B
 EPS = 1e-5
 FLOPS = 2 * C * C * B * NPIX
 
-VJ = {0: [0, 2, 3], 1: [0, 1], 2: [], 3: []}
-GJ = [0, 0, 0, 0, 0, 0, 0, 0]
+NS = [1, 2, 3, 4]
+GP = [0, 0, 2, 2, 2, 2, 2, 2]
+BN_AT = {1: "start", 2: (0, "c")}
+RECIP_AT = {1: (0, "a"), 2: (1, "c"), 3: (4, "b")}
+FILL = [0, 0, 0, 0]
 RUN = 4
+TAIL_SPLIT = True
 
 
 def tile_aattn_pb_t_kernel(tc, content, mean, std, out_w, out_b, out):
     nc = tc.nc
     xv = content.rearrange("b (p j) h w -> b p j (h w)", j=J)
-    mv_ = mean.rearrange("b (p j) h w -> b p j (h w)", j=J)
+    mv = mean.rearrange("b (p j) h w -> b p j (h w)", j=J)
     sv = std.rearrange("b (p j) h w -> b p j (h w)", j=J)
     ov = out.rearrange("b (p j) h w -> b p j (h w)", j=J)
     wv = out_w.rearrange("(m j) c -> m j c", j=J)
@@ -37,6 +41,7 @@ def tile_aattn_pb_t_kernel(tc, content, mean, std, out_w, out_b, out):
 
     with ExitStack() as ctx:
         keep = ctx.enter_context(tc.tile_pool(name="keep", bufs=1))
+        junkp = ctx.enter_context(tc.tile_pool(name="junkp", bufs=4))
         nmp = ctx.enter_context(tc.tile_pool(name="nmp", bufs=4))
         mp = ctx.enter_context(tc.tile_pool(name="mp", bufs=1))
         ogp = ctx.enter_context(tc.tile_pool(name="ogp", bufs=2))
@@ -59,97 +64,95 @@ def tile_aattn_pb_t_kernel(tc, content, mean, std, out_w, out_b, out):
         m_t = [keep.tile([P, J, NPIX], BF16, name="m%d" % b) for b in range(B)]
         w_sb = keep.tile([P, J, C], BF16, name="w_sb")
         b_bf = keep.tile([P, J], BF16, name="b_bf")
-        for j in range(J):
+        for j in (1, 0, 2, 3):
             nc.sync.dma_start(out=x_t[0][:, j, :], in_=xv[0][:, j, :])
         nc.sync.dma_start(out=s_t[0][:], in_=sv[0])
-        nc.sync.dma_start(out=m_t[0][:], in_=mv_[0])
-        nc.sync.dma_start(out=w_sb[:], in_=wv)
+        nc.sync.dma_start(out=m_t[0][:], in_=mv[0])
         nc.sync.dma_start(out=x_t[1][:, 0:2, :], in_=xv[1][:, 0:2, :])
         nc.sync.dma_start(out=x_t[1][:, 2:4, :], in_=xv[1][:, 2:4, :])
+        nc.sync.dma_start(out=w_sb[:], in_=wv)
         nc.sync.dma_start(out=b_bf[:], in_=bv)
         nc.sync.dma_start(out=s_t[1][:], in_=sv[1])
-        nc.sync.dma_start(out=m_t[1][:], in_=mv_[1])
+        nc.sync.dma_start(out=m_t[1][:], in_=mv[1])
         for b in range(2, B):
             nc.sync.dma_start(out=x_t[b][:], in_=xv[b])
             nc.sync.dma_start(out=s_t[b][:], in_=sv[b])
-            nc.sync.dma_start(out=m_t[b][:], in_=mv_[b])
+            nc.sync.dma_start(out=m_t[b][:], in_=mv[b])
 
-        junkp = ctx.enter_context(tc.tile_pool(name="junkp", bufs=4))
         b_f = keep.tile([P, J], F32, name="b_f")
 
+        mu_ap = {}
         rstd_ap = {}
         nbias_ap = {}
-        st8 = {}
+        sd_t = [keep.tile([P, 2, J], F32, name="sd%d" % b) for b in range(B)]
+        rs_t = [keep.tile([P, 2, J], F32, name="rs%d" % b) for b in range(B)]
+        nb_t = [keep.tile([P, J], F32, name="nb%d" % b) for b in range(B)]
+        ag_t = {}
 
-        def stats_scalar(b):
-            js = [j for j in range(J) if j not in VJ[b]]
-            if not js:
-                return
-            n = len(js)
-            sm = keep.tile([P, n], F32, name="sm%d" % b)
-            ng = keep.tile([P, n], F32, name="ng%d" % b)
-            sq = keep.tile([P, n], F32, name="sq%d" % b)
-            sd = keep.tile([P, n], F32, name="sds%d" % b)
-            for k, j in enumerate(js):
+        def sums_scalar(b, rows):
+            if b not in sm_t:
+                sm_t[b] = keep.tile([P, NS[b]], F32, name="sm%d" % b)
+            for j in rows:
                 junk = junkp.tile([P, NPIX], BF16, name="junk")
                 nc.scalar.activation(out=junk[:], in_=x_t[b][:, j, :], func=ACT.Identity,
-                                     accum_out=sm[:, k:k + 1])
-            nc.scalar.mul(out=ng[:], in_=sm[:], mul=-1.0 / NPIX)
-            for k, j in enumerate(js):
+                                     accum_out=sm_t[b][:, j:j + 1])
+
+        def squares_scalar(b):
+            n = NS[b]
+            sq = keep.tile([P, n], F32, name="sq%d" % b)
+            if b == 0:
+                mu = keep.tile([P, n], F32, name="mus%d" % b)
+                nc.scalar.mul(out=mu[:], in_=sm_t[b][:], mul=1.0 / NPIX)
+            for j in range(n):
                 junk = junkp.tile([P, NPIX], BF16, name="junk")
                 nc.scalar.activation(out=junk[:], in_=x_t[b][:, j, :], func=ACT.Square,
-                                     bias=ng[:, k:k + 1], accum_out=sq[:, k:k + 1])
-            nc.scalar.activation(out=sd[:], in_=sq[:], func=ACT.Sqrt,
-                                 scale=1.0 / (NPIX - 1), bias=eps_t[:, 0:1])
-            st8[("s", b)] = (js, ng, sd)
+                                     scale=-float(NPIX), bias=sm_t[b][:, j:j + 1], accum_out=sq[:, j:j + 1])
+                mu_ap[(b, j)] = mu[:, j:j + 1] if b == 0 else sm_t[b][:, j:j + 1]
+            nc.scalar.activation(out=sd_t[b][:, 0, 0:n], in_=sq[:], func=ACT.Sqrt,
+                                 scale=1.0 / (float(NPIX) * NPIX * (NPIX - 1)), bias=eps_t[:, 0:1])
 
         def stats_vector(b):
-            js = VJ[b]
-            if not js:
+            n = J - NS[b]
+            if n == 0:
                 return
-            n = len(js)
             st = keep.tile([P, n, 2, 6], F32, name="st%d" % b)
             ag = keep.tile([P, n, 2], F32, name="ag%d" % b)
-            vv = keep.tile([P, n], F32, name="vv%d" % b)
-            for k, j in enumerate(js):
+            ag_t[b] = ag
+            for k in range(n):
+                j = NS[b] + k
                 for c in range(2):
                     nc.vector.bn_stats(out=st[:, k, c, :], in_=x_t[b][:, j, c * HALF:(c + 1) * HALF])
                 if k > 0:
                     nc.vector.bn_aggr(out=ag[:, k - 1, :], in_=st[:, k - 1, :, :].rearrange("p c s -> p (c s)"))
+                mu_ap[(b, j)] = ag[:, k, 0:1]
             nc.vector.bn_aggr(out=ag[:, n - 1, :], in_=st[:, n - 1, :, :].rearrange("p c s -> p (c s)"))
-            nc.vector.tensor_scalar(out=vv[:], in0=ag[:, :, 1], scalar1=float(NPIX) / (NPIX - 1),
-                                    scalar2=EPS, op0=ALU.mult, op1=ALU.add)
-            st8[("v", b)] = (js, ag, vv)
 
-        def sqrt_vector_group(b):
-            if ("v", b) not in st8:
-                return
-            js, ag, vv = st8[("v", b)]
-            sd = keep.tile([P, len(js)], F32, name="sdv%d" % b)
-            nc.scalar.activation(out=sd[:], in_=vv[:], func=ACT.Sqrt)
-            st8[("v2", b)] = sd
+        def sqrt_vector_rows(b):
+            if b in ag_t:
+                nc.scalar.activation(out=sd_t[b][:, 0, NS[b]:J], in_=ag_t[b][:, :, 1], func=ACT.Sqrt,
+                                     scale=float(NPIX) / (NPIX - 1), bias=eps_t[:, 0:1])
 
-        def chain(b):
-            if ("v", b) in st8:
-                js, ag, vv = st8[("v", b)]
-                sd = st8[("v2", b)]
-                rs = keep.tile([P, len(js)], F32, name="rsv%d" % b)
-                nb = keep.tile([P, len(js)], F32, name="nbv%d" % b)
-                nc.vector.reciprocal(out=rs[:], in_=sd[:])
-                nc.vector.scalar_tensor_tensor(out=nb[:], in0=ag[:, :, 0], scalar=-1.0, in1=rs[:],
-                                               op0=ALU.mult, op1=ALU.mult)
-                for k, j in enumerate(js):
-                    rstd_ap[(b, j)] = rs[:, k:k + 1]
-                    nbias_ap[(b, j)] = nb[:, k:k + 1]
-            if ("s", b) in st8:
-                js, ng, sd = st8[("s", b)]
-                rs = keep.tile([P, len(js)], F32, name="rss%d" % b)
-                nb = keep.tile([P, len(js)], F32, name="nbs%d" % b)
-                nc.vector.reciprocal(out=rs[:], in_=sd[:])
-                nc.vector.tensor_tensor(out=nb[:], in0=ng[:], in1=rs[:], op=ALU.mult)
-                for k, j in enumerate(js):
-                    rstd_ap[(b, j)] = rs[:, k:k + 1]
-                    nbias_ap[(b, j)] = nb[:, k:k + 1]
+        def negate_sd(b):
+            n = NS[b]
+            nc.scalar.mul(out=sd_t[b][:, 1, 0:n], in_=sd_t[b][:, 0, 0:n], mul=-float(NPIX))
+            if n < J:
+                nc.scalar.mul(out=sd_t[b][:, 1, n:J], in_=sd_t[b][:, 0, n:J], mul=-1.0)
+
+        def reciprocal(b, both=True):
+            if both:
+                nc.vector.reciprocal(out=rs_t[b][:], in_=sd_t[b][:])
+            else:
+                nc.vector.reciprocal(out=rs_t[b][:, 0, :], in_=sd_t[b][:, 0, :])
+            for j in range(J):
+                rstd_ap[(b, j)] = rs_t[b][:, 0, j:j + 1]
+
+        def biases(b):
+            for j in range(J):
+                nc.scalar.activation(out=nb_t[b][:, j:j + 1], in_=mu_ap[(b, j)], func=ACT.Identity,
+                                     scale=rs_t[b][:, 1, j:j + 1])
+                nbias_ap[(b, j)] = nb_t[b][:, j:j + 1]
+
+        sm_t = {}
 
         nm_u = {}
         pr_u = {}
@@ -161,11 +164,18 @@ def tile_aattn_pb_t_kernel(tc, content, mean, std, out_w, out_b, out):
             h = u % 2
             return slice(h * HALF, (h + 1) * HALF)
 
+        def centre_row(u, j):
+            if u not in nm_u:
+                nm_u[u] = nmp.tile([P, J, HALF], F32, name="nm")
+            nc.scalar.activation(out=nm_u[u][:, j, :], in_=x_t[0][:, j, cols(u)], func=ACT.Identity,
+                                 scale=-1.0, bias=mu_ap[(0, j)])
+
         def norm(u):
             b = u // 2
             nm = nmp.tile([P, J, HALF], F32, name="nm")
             nm_u[u] = nm
-            for j in range(J):
+            g = GP[u]
+            for j in list(range(J - g, J)) + list(range(J - g)):
                 nc.scalar.activation(out=nm[:, j, :], in_=x_t[b][:, j, cols(u)], func=ACT.Identity,
                                      scale=rstd_ap[(b, j)], bias=nbias_ap[(b, j)])
 
@@ -173,19 +183,19 @@ def tile_aattn_pb_t_kernel(tc, content, mean, std, out_w, out_b, out):
             b = u // 2
             pr = mp.tile([P, J, HALF], F32, name="pr")
             pr_u[u] = pr
-            g = GJ[u]
+            g = GP[u]
             if g:
                 nc.gpsimd.tensor_tensor(out=pr[:, J - g:J, :], in0=nm_u[u][:, J - g:J, :],
                                         in1=s_t[b][:, J - g:J, cols(u)], op=ALU.mult)
 
-        def prod_vector(u, split=False):
+        def prod_vector(u):
             b = u // 2
             pr = pr_u[u]
-            v = J - GJ[u]
-            if split:
-                for j in range(v):
-                    nc.vector.tensor_tensor(out=pr[:, j, :], in0=nm_u[u][:, j, :],
-                                            in1=s_t[b][:, j, cols(u)], op=ALU.mult)
+            v = J - GP[u]
+            if b == 0:
+                for j in range(J):
+                    nc.vector.scalar_tensor_tensor(out=pr[:, j, :], in0=nm_u[u][:, j, :], scalar=rstd_ap[(0, j)],
+                                                   in1=s_t[0][:, j, cols(u)], op0=ALU.mult, op1=ALU.mult)
             else:
                 nc.vector.tensor_tensor(out=pr[:, 0:v, :], in0=nm_u[u][:, 0:v, :],
                                         in1=s_t[b][:, 0:v, cols(u)], op=ALU.mult)
@@ -196,9 +206,9 @@ def tile_aattn_pb_t_kernel(tc, content, mean, std, out_w, out_b, out):
             og_u[u] = og
             nc.vector.tensor_tensor(
                 out=og[:].rearrange("p (c i t) -> p c t i", i=RUN, t=J),
-                in0=pr_u[u][:].rearrange("p t (c i) -> p c t i", i=RUN),
-                in1=m_t[b][:, :, cols(u)].rearrange("p t (c i) -> p c t i", i=RUN),
-                op=ALU.add)
+                in0=m_t[b][:, :, cols(u)].rearrange("p t (c i) -> p c t i", i=RUN),
+                in1=pr_u[u][:].rearrange("p t (c i) -> p c t i", i=RUN),
+                op=(ALU.subtract if b == 0 else ALU.add))
 
         def quantise(u):
             cd = cdp.tile([P, HALF], U32, name="cd", align_bytes=64)
@@ -221,10 +231,14 @@ def tile_aattn_pb_t_kernel(tc, content, mean, std, out_w, out_b, out):
         def finish(u):
             b = u // 2
             ot = otp.tile([P, J, HALF], F32, name="ot")
+            last = TAIL_SPLIT and u == UNITS - 1
             for j in range(J):
                 nc.vector.scalar_tensor_tensor(out=ot[:, j, :], in0=ac_u[u][j][:], scalar=b_f[:, j:j + 1],
                                                in1=x_t[b][:, j, cols(u)], op0=ALU.add, op1=ALU.add)
-            nc.sync.dma_start(out=ov[b][:, :, cols(u)], in_=ot[:])
+                if last and j % 2 == 1:
+                    nc.sync.dma_start(out=ov[b][:, j - 1:j + 1, cols(u)], in_=ot[:, j - 1:j + 1, :])
+            if not last:
+                nc.sync.dma_start(out=ov[b][:, :, cols(u)], in_=ot[:])
 
         w_g = keep.tile([P, C * J], BF16, name="w_g", align_bytes=64)
         w_cd = keep.tile([P, C], U32, name="w_cd", align_bytes=64)
@@ -244,39 +258,60 @@ def tile_aattn_pb_t_kernel(tc, content, mean, std, out_w, out_b, out):
         def weights_quantise():
             nc.vector.quantize_mx(out=w_cd[:].bitcast(FP8X4), scales=w_sc[:], in_=w_g[:])
 
-        stats_scalar(0)
+        def scalar_stats(b):
+            sums_scalar(b, range(FILL[b], NS[b]))
+            squares_scalar(b)
+            sqrt_vector_rows(b)
+            negate_sd(b)
+
+        def hook(where):
+            for b in range(1, B):
+                if BN_AT.get(b) == where:
+                    stats_vector(b)
+                if RECIP_AT[b] == where:
+                    scalar_stats(b)
+                    if b == 1:
+                        weights_transpose()
+                    if b + 1 < B:
+                        sums_scalar(b + 1, range(FILL[b + 1]))
+                    reciprocal(b)
+                    biases(b)
+                    norm(2 * b)
+                    norm(2 * b + 1)
+
+        sums_scalar(0, range(NS[0]))
+        squares_scalar(0)
         stats_vector(0)
-        sqrt_vector_group(0)
-        chain(0)
-        norm(0)
+        centre_row(0, 1)
+        sqrt_vector_rows(0)
+        for j in (0, 2, 3):
+            centre_row(0, j)
+        reciprocal(0, both=False)
         prod_gpsimd(0)
-        prod_vector(0, split=True)
-        norm(1)
-        weights_transpose()
+        prod_vector(0)
+        for j in range(J):
+            centre_row(1, j)
         add_regroup(0)
+        prod_gpsimd(1)
         nc.vector.tensor_copy(out=b_f[:], in_=b_bf[:])
-        stats_vector(1)
-        stats_scalar(1)
-        sqrt_vector_group(1)
+        hook("start")
         for u in range(UNITS):
             nxt = u + 1
             if nxt < UNITS:
-                if nxt not in pr_u:
-                    prod_gpsimd(nxt)
                 prod_vector(nxt)
+            hook((u, "a"))
             if u == 0:
                 weights_quantise()
-            quantise(u)
-            multiply(u)
-            if u % 2 == 0 and u // 2 + 1 < B:
-                b = u // 2 + 1
-                chain(b)
-                norm(2 * b)
-                norm(2 * b + 1)
-                if b + 1 < B:
-                    stats_vector(b + 1)
-                    stats_scalar(b + 1)
-                    sqrt_vector_group(b + 1)
+            if u not in cd_u:
+                quantise(u)
+                multiply(u)
+            hook((u, "b"))
             if nxt < UNITS:
                 add_regroup(nxt)
+            if nxt + 1 < UNITS:
+                prod_gpsimd(nxt + 1)
+            if nxt == UNITS - 1:
+                quantise(nxt)
+                multiply(nxt)
             finish(u)
+            hook((u, "c"))

@@ -22,12 +22,14 @@ EPS = 1e-5
 FLOPS = 2 * C * C * B * NPIX
 
 NS = [1, 2, 3, 4]
-GP = [0, 0, 2, 2, 2, 2, 2, 2]
+GP = [0, 2, 3, 2, 2, 2, 2, 2]
 BN_AT = {1: "start", 2: (0, "c")}
 RECIP_AT = {1: (0, "a"), 2: (1, "c"), 3: (4, "b")}
-FILL = [0, 0, 0, 0]
+FILL = [0, 0, 0, 1]
 RUN = 4
 TAIL_SPLIT = True
+HEAD_G = True
+TAIL_G = True
 
 
 def tile_aattn_pb_t_kernel(tc, content, mean, std, out_w, out_b, out):
@@ -66,12 +68,13 @@ def tile_aattn_pb_t_kernel(tc, content, mean, std, out_w, out_b, out):
         b_bf = keep.tile([P, J], BF16, name="b_bf")
         for j in (1, 0, 2, 3):
             nc.sync.dma_start(out=x_t[0][:, j, :], in_=xv[0][:, j, :])
+        nc.sync.dma_start(out=b_bf[:], in_=bv)
         nc.sync.dma_start(out=s_t[0][:], in_=sv[0])
-        nc.sync.dma_start(out=m_t[0][:], in_=mv[0])
         nc.sync.dma_start(out=x_t[1][:, 0:2, :], in_=xv[1][:, 0:2, :])
+        nc.sync.dma_start(out=m_t[0][:, :, 0:HALF], in_=mv[0][:, :, 0:HALF])
+        nc.sync.dma_start(out=m_t[0][:, :, HALF:NPIX], in_=mv[0][:, :, HALF:NPIX])
         nc.sync.dma_start(out=x_t[1][:, 2:4, :], in_=xv[1][:, 2:4, :])
         nc.sync.dma_start(out=w_sb[:], in_=wv)
-        nc.sync.dma_start(out=b_bf[:], in_=bv)
         nc.sync.dma_start(out=s_t[1][:], in_=sv[1])
         nc.sync.dma_start(out=m_t[1][:], in_=mv[1])
         for b in range(2, B):
@@ -164,11 +167,30 @@ def tile_aattn_pb_t_kernel(tc, content, mean, std, out_w, out_b, out):
             h = u % 2
             return slice(h * HALF, (h + 1) * HALF)
 
+        nm0 = keep.tile([P, J, NPIX], F32, name="nm0")
+        nm_u[0] = nm0[:, :, 0:HALF]
+        nm_u[1] = nm0[:, :, HALF:NPIX]
+
         def centre_row(u, j):
-            if u not in nm_u:
-                nm_u[u] = nmp.tile([P, J, HALF], F32, name="nm")
             nc.scalar.activation(out=nm_u[u][:, j, :], in_=x_t[0][:, j, cols(u)], func=ACT.Identity,
                                  scale=-1.0, bias=mu_ap[(0, j)])
+
+        def centre_row_gpsimd(j):
+            nc.gpsimd.tensor_scalar(out=nm0[:, j, :], in0=x_t[0][:, j, :], scalar1=-1.0,
+                                    scalar2=mu_ap[(0, j)], op0=ALU.mult, op1=ALU.add)
+
+        def minus_norm_rows(u, rows):
+            lo = rows[0]
+            hi = rows[-1] + 1
+            nrs = keep.tile([P, J], F32, name="nrs0")
+            pb = keep.tile([P, J], F32, name="pb0")
+            nc.scalar.mul(out=nrs[:, lo:hi], in_=rs_t[0][:, 0, lo:hi], mul=-1.0)
+            for j in rows:
+                nc.scalar.activation(out=pb[:, j:j + 1], in_=mu_ap[(0, j)], func=ACT.Identity,
+                                     scale=rs_t[0][:, 0, j:j + 1])
+            for j in rows:
+                nc.scalar.activation(out=nm_u[u][:, j, :], in_=x_t[0][:, j, cols(u)], func=ACT.Identity,
+                                     scale=nrs[:, j:j + 1], bias=pb[:, j:j + 1])
 
         def norm(u):
             b = u // 2
@@ -193,7 +215,7 @@ def tile_aattn_pb_t_kernel(tc, content, mean, std, out_w, out_b, out):
             pr = pr_u[u]
             v = J - GP[u]
             if b == 0:
-                for j in range(J):
+                for j in range(v):
                     nc.vector.scalar_tensor_tensor(out=pr[:, j, :], in0=nm_u[u][:, j, :], scalar=rstd_ap[(0, j)],
                                                    in1=s_t[0][:, j, cols(u)], op0=ALU.mult, op1=ALU.mult)
             else:
@@ -218,26 +240,36 @@ def tile_aattn_pb_t_kernel(tc, content, mean, std, out_w, out_b, out):
 
         def multiply(u):
             cd, sc = cd_u[u]
-            accs = []
-            for j in range(J):
+            accs = {}
+            for j in ((3, 0, 1, 2) if TAIL_G and u == UNITS - 1 else range(J)):
                 acc = psum.tile([P, HALF], F32, name="acc", tag="bank")
                 nc.tensor.matmul_mx(out=acc[:], lhsT=w_cd[:, j * P:(j + 1) * P].bitcast(FP8X4),
                                     lhsT_scale=w_sc[:, j * P:(j + 1) * P],
                                     rhs=cd[:].bitcast(FP8X4), rhs_scale=sc[:],
                                     start=True, stop=True)
-                accs.append(acc)
+                accs[j] = acc
             ac_u[u] = accs
+
+        yt_box = {}
 
         def finish(u):
             b = u // 2
             ot = otp.tile([P, J, HALF], F32, name="ot")
-            last = TAIL_SPLIT and u == UNITS - 1
-            for j in range(J):
+            helped = TAIL_G and u >= UNITS - 2
+            if helped:
+                if "yt" not in yt_box:
+                    yt_box["yt"] = mp.tile([P, 2, HALF], F32, name="yt", tag="pr")
+                yt = yt_box["yt"]
+                k = u - (UNITS - 2)
+                nc.scalar.activation(out=yt[:, k, :], in_=ac_u[u][3][:], func=ACT.Identity, bias=b_f[:, 3:4])
+                nc.gpsimd.tensor_tensor(out=ot[:, 3, :], in0=yt[:, k, :], in1=x_t[b][:, 3, cols(u)], op=ALU.add)
+            for j in range(3 if helped else J):
                 nc.vector.scalar_tensor_tensor(out=ot[:, j, :], in0=ac_u[u][j][:], scalar=b_f[:, j:j + 1],
                                                in1=x_t[b][:, j, cols(u)], op0=ALU.add, op1=ALU.add)
-                if last and j % 2 == 1:
-                    nc.sync.dma_start(out=ov[b][:, j - 1:j + 1, cols(u)], in_=ot[:, j - 1:j + 1, :])
-            if not last:
+            if helped:
+                nc.sync.dma_start(out=ov[b][:, 0:3, cols(u)], in_=ot[:, 0:3, :])
+                nc.sync.dma_start(out=ov[b][:, 3:4, cols(u)], in_=ot[:, 3:4, :])
+            else:
                 nc.sync.dma_start(out=ov[b][:, :, cols(u)], in_=ot[:])
 
         w_g = keep.tile([P, C * J], BF16, name="w_g", align_bytes=64)
@@ -261,6 +293,8 @@ def tile_aattn_pb_t_kernel(tc, content, mean, std, out_w, out_b, out):
         def scalar_stats(b):
             sums_scalar(b, range(FILL[b], NS[b]))
             squares_scalar(b)
+            if b == 1:
+                weights_transpose()
             sqrt_vector_rows(b)
             negate_sd(b)
 
@@ -270,8 +304,6 @@ def tile_aattn_pb_t_kernel(tc, content, mean, std, out_w, out_b, out):
                     stats_vector(b)
                 if RECIP_AT[b] == where:
                     scalar_stats(b)
-                    if b == 1:
-                        weights_transpose()
                     if b + 1 < B:
                         sums_scalar(b + 1, range(FILL[b + 1]))
                     reciprocal(b)
@@ -282,28 +314,28 @@ def tile_aattn_pb_t_kernel(tc, content, mean, std, out_w, out_b, out):
         sums_scalar(0, range(NS[0]))
         squares_scalar(0)
         stats_vector(0)
-        centre_row(0, 1)
+        centre_row_gpsimd(0)
+        centre_row_gpsimd(1)
         sqrt_vector_rows(0)
-        for j in (0, 2, 3):
-            centre_row(0, j)
+        centre_row(0, 2)
+        centre_row(0, 3)
         reciprocal(0, both=False)
         prod_gpsimd(0)
         prod_vector(0)
-        for j in range(J):
-            centre_row(1, j)
+        nc.vector.tensor_copy(out=b_f[:], in_=b_bf[:])
+        minus_norm_rows(1, [2, 3])
         add_regroup(0)
         prod_gpsimd(1)
-        nc.vector.tensor_copy(out=b_f[:], in_=b_bf[:])
         hook("start")
         for u in range(UNITS):
             nxt = u + 1
             if nxt < UNITS:
                 prod_vector(nxt)
             hook((u, "a"))
-            if u == 0:
-                weights_quantise()
             if u not in cd_u:
                 quantise(u)
+                if u == 0:
+                    weights_quantise()
                 multiply(u)
             hook((u, "b"))
             if nxt < UNITS:

@@ -21,11 +21,12 @@ UNITS = 2 * B
 EPS = 1e-5
 FLOPS = 2 * C * C * B * NPIX
 
-NS = [1, 2, 3, 4]
-GP = [0, 2, 3, 2, 2, 2, 2, 2]
-BN_AT = {1: "start", 2: (0, "c")}
-RECIP_AT = {1: (0, "a"), 2: (1, "c"), 3: (4, "b")}
-FILL = [0, 0, 0, 1]
+NS = [1, 2, 3, 3]
+GP = [0, 2, 0, 0, 0, 0, 0, 0]
+VC = [0, 0, 96, 192, 96, 192, 192, 192]
+BN_AT = {1: "start", 2: (0, "c"), 3: (2, "c")}
+RECIP_AT = {1: (0, "a"), 2: (2, "a"), 3: (4, "a")}
+FILL = [0, 0, 0, 0]
 RUN = 4
 TAIL_SPLIT = True
 HEAD_G = True
@@ -60,6 +61,8 @@ def tile_aattn_pb_t_kernel(tc, content, mean, std, out_w, out_b, out):
         nc.scalar.activation(out=warm_t[:], in_=one_t[:], func=ACT.Sqrt)
         ident = keep.tile([P, P], F32, name="ident")
         make_identity(nc, ident[:])
+        ident_bf = keep.tile([P, P], BF16, name="ident_bf")
+        make_identity(nc, ident_bf[:])
 
         x_t = [keep.tile([P, J, NPIX], BF16, name="x%d" % b) for b in range(B)]
         s_t = [keep.tile([P, J, NPIX], BF16, name="s%d" % b) for b in range(B)]
@@ -196,19 +199,37 @@ def tile_aattn_pb_t_kernel(tc, content, mean, std, out_w, out_b, out):
             b = u // 2
             nm = nmp.tile([P, J, HALF], F32, name="nm")
             nm_u[u] = nm
-            g = GP[u]
-            for j in list(range(J - g, J)) + list(range(J - g)):
-                nc.scalar.activation(out=nm[:, j, :], in_=x_t[b][:, j, cols(u)], func=ACT.Identity,
-                                     scale=rstd_ap[(b, j)], bias=nbias_ap[(b, j)])
+            c0 = (u % 2) * HALF
+            for lo, hi in ((VC[u], HALF), (0, VC[u])):
+                for j in range(J):
+                    nc.scalar.activation(out=nm[:, j, lo:hi], in_=x_t[b][:, j, c0 + lo:c0 + hi], func=ACT.Identity,
+                                         scale=rstd_ap[(b, j)], bias=nbias_ap[(b, j)])
+
+        st_u = {}
+
+        def stage_std(u):
+            b = u // 2
+            c0 = (u % 2) * HALF
+            st_u[u] = []
+            for h in range(2):
+                st = psum.tile([P, 2, VC[u]], F32, name="st", tag="bank")
+                for r in range(2):
+                    nc.tensor.matmul(out=st[:, r, :], lhsT=ident_bf[:], rhs=s_t[b][:, 2 * h + r, c0:c0 + VC[u]],
+                                     start=True, stop=True)
+                st_u[u].append(st)
 
         def prod_gpsimd(u):
             b = u // 2
             pr = mp.tile([P, J, HALF], F32, name="pr")
             pr_u[u] = pr
             g = GP[u]
+            c0 = (u % 2) * HALF
             if g:
                 nc.gpsimd.tensor_tensor(out=pr[:, J - g:J, :], in0=nm_u[u][:, J - g:J, :],
                                         in1=s_t[b][:, J - g:J, cols(u)], op=ALU.mult)
+            if VC[u]:
+                nc.gpsimd.tensor_tensor(out=pr[:, :, VC[u]:HALF], in0=nm_u[u][:, :, VC[u]:HALF],
+                                        in1=s_t[b][:, :, c0 + VC[u]:c0 + HALF], op=ALU.mult)
 
         def prod_vector(u):
             b = u // 2
@@ -219,8 +240,9 @@ def tile_aattn_pb_t_kernel(tc, content, mean, std, out_w, out_b, out):
                     nc.vector.scalar_tensor_tensor(out=pr[:, j, :], in0=nm_u[u][:, j, :], scalar=rstd_ap[(0, j)],
                                                    in1=s_t[0][:, j, cols(u)], op0=ALU.mult, op1=ALU.mult)
             else:
-                nc.vector.tensor_tensor(out=pr[:, 0:v, :], in0=nm_u[u][:, 0:v, :],
-                                        in1=s_t[b][:, 0:v, cols(u)], op=ALU.mult)
+                for h in range(2):
+                    nc.vector.tensor_tensor(out=pr[:, 2 * h:2 * h + 2, 0:VC[u]], in0=nm_u[u][:, 2 * h:2 * h + 2, 0:VC[u]],
+                                            in1=st_u[u][h][:], op=ALU.mult)
 
         def add_regroup(u):
             b = u // 2
@@ -263,12 +285,19 @@ def tile_aattn_pb_t_kernel(tc, content, mean, std, out_w, out_b, out):
                 k = u - (UNITS - 2)
                 nc.scalar.activation(out=yt[:, k, :], in_=ac_u[u][3][:], func=ACT.Identity, bias=b_f[:, 3:4])
                 nc.gpsimd.tensor_tensor(out=ot[:, 3, :], in0=yt[:, k, :], in1=x_t[b][:, 3, cols(u)], op=ALU.add)
+            last = u == UNITS - 1
             for j in range(3 if helped else J):
                 nc.vector.scalar_tensor_tensor(out=ot[:, j, :], in0=ac_u[u][j][:], scalar=b_f[:, j:j + 1],
                                                in1=x_t[b][:, j, cols(u)], op0=ALU.add, op1=ALU.add)
+                if last and j == 1:
+                    nc.sync.dma_start(out=ov[b][:, 0:2, cols(u)], in_=ot[:, 0:2, :])
             if helped:
-                nc.sync.dma_start(out=ov[b][:, 0:3, cols(u)], in_=ot[:, 0:3, :])
-                nc.sync.dma_start(out=ov[b][:, 3:4, cols(u)], in_=ot[:, 3:4, :])
+                if last:
+                    nc.sync.dma_start(out=ov[b][:, 3:4, cols(u)], in_=ot[:, 3:4, :])
+                    nc.sync.dma_start(out=ov[b][:, 2:3, cols(u)], in_=ot[:, 2:3, :])
+                else:
+                    nc.sync.dma_start(out=ov[b][:, 0:3, cols(u)], in_=ot[:, 0:3, :])
+                    nc.sync.dma_start(out=ov[b][:, 3:4, cols(u)], in_=ot[:, 3:4, :])
             else:
                 nc.sync.dma_start(out=ov[b][:, :, cols(u)], in_=ot[:])
 
@@ -337,6 +366,8 @@ def tile_aattn_pb_t_kernel(tc, content, mean, std, out_w, out_b, out):
                 if u == 0:
                     weights_quantise()
                 multiply(u)
+            if u + 2 < UNITS:
+                stage_std(u + 2)
             hook((u, "b"))
             if nxt < UNITS:
                 add_regroup(nxt)

@@ -25,12 +25,13 @@ NS = [1, 2, 3, 3]
 GP = [0, 2, 0, 0, 0, 0, 0, 0]
 VC = [0, 0, 96, 192, 96, 192, 192, 192]
 BN_AT = {1: "start", 2: (0, "c"), 3: (2, "c")}
-RECIP_AT = {1: (0, "a"), 2: (2, "a"), 3: (4, "a")}
+RECIP_AT = {1: (0, "a"), 2: (2, "a"), 3: (4, "b")}
 FILL = [0, 0, 0, 0]
 RUN = 4
 TAIL_SPLIT = True
+EARLY6 = 0
 HEAD_G = True
-TAIL_G = True
+TAIL_G = False
 
 
 def tile_aattn_pb_t_kernel(tc, content, mean, std, out_w, out_b, out):
@@ -71,13 +72,13 @@ def tile_aattn_pb_t_kernel(tc, content, mean, std, out_w, out_b, out):
         b_bf = keep.tile([P, J], BF16, name="b_bf")
         for j in (1, 0, 2, 3):
             nc.sync.dma_start(out=x_t[0][:, j, :], in_=xv[0][:, j, :])
-        nc.sync.dma_start(out=b_bf[:], in_=bv)
         nc.sync.dma_start(out=s_t[0][:], in_=sv[0])
         nc.sync.dma_start(out=x_t[1][:, 0:2, :], in_=xv[1][:, 0:2, :])
         nc.sync.dma_start(out=m_t[0][:, :, 0:HALF], in_=mv[0][:, :, 0:HALF])
         nc.sync.dma_start(out=m_t[0][:, :, HALF:NPIX], in_=mv[0][:, :, HALF:NPIX])
         nc.sync.dma_start(out=x_t[1][:, 2:4, :], in_=xv[1][:, 2:4, :])
         nc.sync.dma_start(out=w_sb[:], in_=wv)
+        nc.sync.dma_start(out=b_bf[:], in_=bv)
         nc.sync.dma_start(out=s_t[1][:], in_=sv[1])
         nc.sync.dma_start(out=m_t[1][:], in_=mv[1])
         for b in range(2, B):
@@ -117,6 +118,10 @@ def tile_aattn_pb_t_kernel(tc, content, mean, std, out_w, out_b, out):
             nc.scalar.activation(out=sd_t[b][:, 0, 0:n], in_=sq[:], func=ACT.Sqrt,
                                  scale=1.0 / (float(NPIX) * NPIX * (NPIX - 1)), bias=eps_t[:, 0:1])
 
+        def aggregate(b, k):
+            st, ag = st_t[b]
+            nc.vector.bn_aggr(out=ag[:, k, :], in_=st[:, k, :, :].rearrange("p c s -> p (c s)"))
+
         def stats_vector(b):
             n = J - NS[b]
             if n == 0:
@@ -124,14 +129,18 @@ def tile_aattn_pb_t_kernel(tc, content, mean, std, out_w, out_b, out):
             st = keep.tile([P, n, 2, 6], F32, name="st%d" % b)
             ag = keep.tile([P, n, 2], F32, name="ag%d" % b)
             ag_t[b] = ag
+            st_t[b] = (st, ag)
             for k in range(n):
                 j = NS[b] + k
                 for c in range(2):
                     nc.vector.bn_stats(out=st[:, k, c, :], in_=x_t[b][:, j, c * HALF:(c + 1) * HALF])
-                if k > 0:
-                    nc.vector.bn_aggr(out=ag[:, k - 1, :], in_=st[:, k - 1, :, :].rearrange("p c s -> p (c s)"))
+                    if c == 0 and k > 0:
+                        aggregate(b, k - 1)
                 mu_ap[(b, j)] = ag[:, k, 0:1]
-            nc.vector.bn_aggr(out=ag[:, n - 1, :], in_=st[:, n - 1, :, :].rearrange("p c s -> p (c s)"))
+            if n > 1:
+                aggregate(b, n - 1)
+            else:
+                late_aggr[b] = True
 
         def sqrt_vector_rows(b):
             if b in ag_t:
@@ -159,6 +168,8 @@ def tile_aattn_pb_t_kernel(tc, content, mean, std, out_w, out_b, out):
                 nbias_ap[(b, j)] = nb_t[b][:, j:j + 1]
 
         sm_t = {}
+        st_t = {}
+        late_aggr = {}
 
         nm_u = {}
         pr_u = {}
@@ -236,7 +247,7 @@ def tile_aattn_pb_t_kernel(tc, content, mean, std, out_w, out_b, out):
             pr = pr_u[u]
             v = J - GP[u]
             if b == 0:
-                for j in range(v):
+                for j in ((1, 0, 2, 3) if v == J else range(v)):
                     nc.vector.scalar_tensor_tensor(out=pr[:, j, :], in0=nm_u[u][:, j, :], scalar=rstd_ap[(0, j)],
                                                    in1=s_t[0][:, j, cols(u)], op0=ALU.mult, op1=ALU.mult)
             else:
@@ -274,47 +285,56 @@ def tile_aattn_pb_t_kernel(tc, content, mean, std, out_w, out_b, out):
 
         yt_box = {}
 
+        ot_u = {}
+
+        def exit_tile(u):
+            if u not in ot_u:
+                ot_u[u] = otp.tile([P, J, HALF], F32, name="ot")
+            return ot_u[u]
+
+        def exit_bank(u, j, store):
+            b = u // 2
+            ot = exit_tile(u)
+            nc.vector.scalar_tensor_tensor(out=ot[:, j, :], in0=ac_u[u][j][:], scalar=b_f[:, j:j + 1],
+                                           in1=x_t[b][:, j, cols(u)], op0=ALU.add, op1=ALU.add)
+            if store:
+                nc.sync.dma_start(out=ov[b][:, j:j + 1, cols(u)], in_=ot[:, j:j + 1, :])
+
+        def exit_bank_helped(u):
+            b = u // 2
+            ot = exit_tile(u)
+            if "yt" not in yt_box:
+                yt_box["yt"] = mp.tile([P, 2, HALF], F32, name="yt", tag="pr")
+            yt = yt_box["yt"]
+            k = u - (UNITS - 2)
+            nc.scalar.activation(out=yt[:, k, :], in_=ac_u[u][3][:], func=ACT.Identity, bias=b_f[:, 3:4])
+            nc.gpsimd.tensor_tensor(out=ot[:, 3, :], in0=yt[:, k, :], in1=x_t[b][:, 3, cols(u)], op=ALU.add)
+
         def finish(u):
             b = u // 2
-            ot = otp.tile([P, J, HALF], F32, name="ot")
-            helped = TAIL_G and u >= UNITS - 2
-            if helped:
-                if "yt" not in yt_box:
-                    yt_box["yt"] = mp.tile([P, 2, HALF], F32, name="yt", tag="pr")
-                yt = yt_box["yt"]
-                k = u - (UNITS - 2)
-                nc.scalar.activation(out=yt[:, k, :], in_=ac_u[u][3][:], func=ACT.Identity, bias=b_f[:, 3:4])
-                nc.gpsimd.tensor_tensor(out=ot[:, 3, :], in0=yt[:, k, :], in1=x_t[b][:, 3, cols(u)], op=ALU.add)
-            last = u == UNITS - 1
-            for j in range(3 if helped else J):
-                nc.vector.scalar_tensor_tensor(out=ot[:, j, :], in0=ac_u[u][j][:], scalar=b_f[:, j:j + 1],
-                                               in1=x_t[b][:, j, cols(u)], op0=ALU.add, op1=ALU.add)
-                if last and j == 1:
-                    nc.sync.dma_start(out=ov[b][:, 0:2, cols(u)], in_=ot[:, 0:2, :])
-            if helped:
-                if last:
-                    nc.sync.dma_start(out=ov[b][:, 3:4, cols(u)], in_=ot[:, 3:4, :])
-                    nc.sync.dma_start(out=ov[b][:, 2:3, cols(u)], in_=ot[:, 2:3, :])
-                else:
-                    nc.sync.dma_start(out=ov[b][:, 0:3, cols(u)], in_=ot[:, 0:3, :])
-                    nc.sync.dma_start(out=ov[b][:, 3:4, cols(u)], in_=ot[:, 3:4, :])
-            else:
-                nc.sync.dma_start(out=ov[b][:, :, cols(u)], in_=ot[:])
+            for j in range(J):
+                exit_bank(u, j, False)
+            nc.sync.dma_start(out=ov[b][:, :, cols(u)], in_=ot_u[u][:])
 
         w_g = keep.tile([P, C * J], BF16, name="w_g", align_bytes=64)
         w_cd = keep.tile([P, C], U32, name="w_cd", align_bytes=64)
         w_sc = keep.tile([P, C], U8, name="w_sc", align_bytes=64)
 
+        wt_h = []
+
         def weights_transpose():
             w32 = w_sb[:].bitcast(F32).rearrange("p j (q u) -> p j q u", u=2)
-            g32 = w_g[:].bitcast(F32)
             for hh in range(2):
                 wt = psum.tile([P, 2, 2, P], F32, name="wt", tag="bank")
                 for a in range(2):
                     for u2 in range(2):
                         nc.tensor.transpose(wt[:, a, u2, :], w32[:, 2 * hh + a, :, u2], ident[:])
-                nc.scalar.copy(out=g32[:, hh * 512:(hh + 1) * 512].rearrange("p (a m u) -> p a m u", a=2, u=2),
-                               in_=wt[:].rearrange("p a u m -> p a m u"))
+                wt_h.append(wt)
+
+        def weights_copy(hh):
+            g32 = w_g[:].bitcast(F32)
+            nc.scalar.copy(out=g32[:, hh * 512:(hh + 1) * 512].rearrange("p (a m u) -> p a m u", a=2, u=2),
+                           in_=wt_h[hh][:].rearrange("p a u m -> p a m u"))
 
         def weights_quantise():
             nc.vector.quantize_mx(out=w_cd[:].bitcast(FP8X4), scales=w_sc[:], in_=w_g[:])
@@ -324,8 +344,11 @@ def tile_aattn_pb_t_kernel(tc, content, mean, std, out_w, out_b, out):
             squares_scalar(b)
             if b == 1:
                 weights_transpose()
+                weights_copy(0)
             sqrt_vector_rows(b)
             negate_sd(b)
+            if b == 1:
+                weights_copy(1)
 
         def hook(where):
             for b in range(1, B):
@@ -343,15 +366,14 @@ def tile_aattn_pb_t_kernel(tc, content, mean, std, out_w, out_b, out):
         sums_scalar(0, range(NS[0]))
         squares_scalar(0)
         stats_vector(0)
-        centre_row_gpsimd(0)
         centre_row_gpsimd(1)
+        centre_row_gpsimd(0)
         sqrt_vector_rows(0)
         centre_row(0, 2)
         centre_row(0, 3)
         reciprocal(0, both=False)
         prod_gpsimd(0)
         prod_vector(0)
-        nc.vector.tensor_copy(out=b_f[:], in_=b_bf[:])
         minus_norm_rows(1, [2, 3])
         add_regroup(0)
         prod_gpsimd(1)
@@ -360,15 +382,23 @@ def tile_aattn_pb_t_kernel(tc, content, mean, std, out_w, out_b, out):
             nxt = u + 1
             if nxt < UNITS:
                 prod_vector(nxt)
+            for b in range(B):
+                if late_aggr.get(b):
+                    aggregate(b, 0)
+                    late_aggr[b] = False
             hook((u, "a"))
             if u not in cd_u:
                 quantise(u)
                 if u == 0:
                     weights_quantise()
+                    nc.vector.tensor_copy(out=b_f[:], in_=b_bf[:])
                 multiply(u)
             if u + 2 < UNITS:
                 stage_std(u + 2)
             hook((u, "b"))
+            if u == UNITS - 2:
+                for j in range(EARLY6):
+                    exit_bank(u, j, True)
             if nxt < UNITS:
                 add_regroup(nxt)
             if nxt + 1 < UNITS:
@@ -376,5 +406,13 @@ def tile_aattn_pb_t_kernel(tc, content, mean, std, out_w, out_b, out):
             if nxt == UNITS - 1:
                 quantise(nxt)
                 multiply(nxt)
-            finish(u)
+            if u < UNITS - 2:
+                finish(u)
+            else:
+                if TAIL_G:
+                    exit_bank_helped(u)
+                for j in range(EARLY6 if u == UNITS - 2 else 0, 3 if TAIL_G else J):
+                    exit_bank(u, j, True)
+                if TAIL_G:
+                    nc.sync.dma_start(out=ov[u // 2][:, 3:4, cols(u)], in_=ot_u[u][:, 3:4, :])
             hook((u, "c"))

@@ -23,13 +23,16 @@ FLOPS = 2 * C * C * B * NPIX
 
 NS = [1, 2, 3, 3]
 GP = [0, 2, 0, 0, 0, 0, 0, 0]
-VC = [0, 0, 96, 192, 96, 192, 192, 192]
+VC = [0, 0, 128, 224, 128, 224, 224, 224]
 BN_AT = {1: "start", 2: (0, "c"), 3: (2, "c")}
 RECIP_AT = {1: (0, "a"), 2: (2, "a"), 3: (4, "b")}
 FILL = [0, 0, 0, 0]
 RUN = 4
 TAIL_SPLIT = True
 EARLY6 = 0
+G_CENTRE = [(1, 0, 1024), (0, 0, 512)]
+S_CENTRE_A = []
+S_CENTRE_B = [(1, 0)]
 HEAD_G = True
 TAIL_G = False
 
@@ -72,12 +75,13 @@ def tile_aattn_pb_t_kernel(tc, content, mean, std, out_w, out_b, out):
         b_bf = keep.tile([P, J], BF16, name="b_bf")
         for j in (1, 0, 2, 3):
             nc.sync.dma_start(out=x_t[0][:, j, :], in_=xv[0][:, j, :])
-        nc.sync.dma_start(out=s_t[0][:], in_=sv[0])
+        nc.sync.dma_start(out=s_t[0][:, :, 0:HALF], in_=sv[0][:, :, 0:HALF])
         nc.sync.dma_start(out=x_t[1][:, 0:2, :], in_=xv[1][:, 0:2, :])
         nc.sync.dma_start(out=m_t[0][:, :, 0:HALF], in_=mv[0][:, :, 0:HALF])
-        nc.sync.dma_start(out=m_t[0][:, :, HALF:NPIX], in_=mv[0][:, :, HALF:NPIX])
         nc.sync.dma_start(out=x_t[1][:, 2:4, :], in_=xv[1][:, 2:4, :])
+        nc.sync.dma_start(out=s_t[0][:, :, HALF:NPIX], in_=sv[0][:, :, HALF:NPIX])
         nc.sync.dma_start(out=w_sb[:], in_=wv)
+        nc.sync.dma_start(out=m_t[0][:, :, HALF:NPIX], in_=mv[0][:, :, HALF:NPIX])
         nc.sync.dma_start(out=b_bf[:], in_=bv)
         nc.sync.dma_start(out=s_t[1][:], in_=sv[1])
         nc.sync.dma_start(out=m_t[1][:], in_=mv[1])
@@ -189,8 +193,8 @@ def tile_aattn_pb_t_kernel(tc, content, mean, std, out_w, out_b, out):
             nc.scalar.activation(out=nm_u[u][:, j, :], in_=x_t[0][:, j, cols(u)], func=ACT.Identity,
                                  scale=-1.0, bias=mu_ap[(0, j)])
 
-        def centre_row_gpsimd(j):
-            nc.gpsimd.tensor_scalar(out=nm0[:, j, :], in0=x_t[0][:, j, :], scalar1=-1.0,
+        def centre_gpsimd(j, lo, hi):
+            nc.gpsimd.tensor_scalar(out=nm0[:, j, lo:hi], in0=x_t[0][:, j, lo:hi], scalar1=-1.0,
                                     scalar2=mu_ap[(0, j)], op0=ALU.mult, op1=ALU.add)
 
         def minus_norm_rows(u, rows):
@@ -366,8 +370,10 @@ def tile_aattn_pb_t_kernel(tc, content, mean, std, out_w, out_b, out):
         sums_scalar(0, range(NS[0]))
         squares_scalar(0)
         stats_vector(0)
-        centre_row_gpsimd(1)
-        centre_row_gpsimd(0)
+        for j, lo, hi in G_CENTRE:
+            centre_gpsimd(j, lo, hi)
+        for u, j in S_CENTRE_A:
+            centre_row(u, j)
         sqrt_vector_rows(0)
         centre_row(0, 2)
         centre_row(0, 3)
@@ -375,6 +381,8 @@ def tile_aattn_pb_t_kernel(tc, content, mean, std, out_w, out_b, out):
         prod_gpsimd(0)
         prod_vector(0)
         minus_norm_rows(1, [2, 3])
+        for u, j in S_CENTRE_B:
+            centre_row(u, j)
         add_regroup(0)
         prod_gpsimd(1)
         hook("start")

@@ -23,16 +23,13 @@ FLOPS = 2 * C * C * B * NPIX
 
 NS = [1, 2, 3, 3]
 GP = [0, 2, 0, 0, 0, 0, 0, 0]
-VC = [0, 0, 128, 224, 128, 224, 224, 224]
+VC = [0, 0, 96, 192, 96, 192, 192, 192]
 BN_AT = {1: "start", 2: (0, "c"), 3: (2, "c")}
 RECIP_AT = {1: (0, "a"), 2: (2, "a"), 3: (4, "b")}
 FILL = [0, 0, 0, 0]
 RUN = 4
 TAIL_SPLIT = True
 EARLY6 = 0
-G_CENTRE = [(1, 0, 1024), (0, 0, 512)]
-S_CENTRE_A = []
-S_CENTRE_B = [(1, 0)]
 HEAD_G = True
 TAIL_G = False
 
@@ -69,19 +66,27 @@ def tile_aattn_pb_t_kernel(tc, content, mean, std, out_w, out_b, out):
         make_identity(nc, ident_bf[:])
 
         x_t = [keep.tile([P, J, NPIX], BF16, name="x%d" % b) for b in range(B)]
-        s_t = [keep.tile([P, J, NPIX], BF16, name="s%d" % b) for b in range(B)]
-        m_t = [keep.tile([P, J, NPIX], BF16, name="m%d" % b) for b in range(B)]
+        s_t = [None] + [keep.tile([P, J, NPIX], BF16, name="s%d" % b) for b in range(1, B)]
+        m_t = [None] + [keep.tile([P, J, NPIX], BF16, name="m%d" % b) for b in range(1, B)]
+        s0_h = [keep.tile([P, J, HALF], BF16, name="s0h%d" % h) for h in range(2)]
+        m0_h = [keep.tile([P, J, HALF], BF16, name="m0h%d" % h) for h in range(2)]
+
+        def std_of(u):
+            return s0_h[u][:] if u < 2 else s_t[u // 2][:, :, (u % 2) * HALF:(u % 2 + 1) * HALF]
+
+        def mean_of(u):
+            return m0_h[u][:] if u < 2 else m_t[u // 2][:, :, (u % 2) * HALF:(u % 2 + 1) * HALF]
         w_sb = keep.tile([P, J, C], BF16, name="w_sb")
         b_bf = keep.tile([P, J], BF16, name="b_bf")
         for j in (1, 0, 2, 3):
             nc.sync.dma_start(out=x_t[0][:, j, :], in_=xv[0][:, j, :])
-        nc.sync.dma_start(out=s_t[0][:, :, 0:HALF], in_=sv[0][:, :, 0:HALF])
+        nc.sync.dma_start(out=s0_h[0][:], in_=sv[0][:, :, 0:HALF])
         nc.sync.dma_start(out=x_t[1][:, 0:2, :], in_=xv[1][:, 0:2, :])
-        nc.sync.dma_start(out=m_t[0][:, :, 0:HALF], in_=mv[0][:, :, 0:HALF])
+        nc.sync.dma_start(out=m0_h[0][:], in_=mv[0][:, :, 0:HALF])
         nc.sync.dma_start(out=x_t[1][:, 2:4, :], in_=xv[1][:, 2:4, :])
-        nc.sync.dma_start(out=s_t[0][:, :, HALF:NPIX], in_=sv[0][:, :, HALF:NPIX])
+        nc.sync.dma_start(out=s0_h[1][:], in_=sv[0][:, :, HALF:NPIX])
         nc.sync.dma_start(out=w_sb[:], in_=wv)
-        nc.sync.dma_start(out=m_t[0][:, :, HALF:NPIX], in_=mv[0][:, :, HALF:NPIX])
+        nc.sync.dma_start(out=m0_h[1][:], in_=mv[0][:, :, HALF:NPIX])
         nc.sync.dma_start(out=b_bf[:], in_=bv)
         nc.sync.dma_start(out=s_t[1][:], in_=sv[1])
         nc.sync.dma_start(out=m_t[1][:], in_=mv[1])
@@ -193,8 +198,8 @@ def tile_aattn_pb_t_kernel(tc, content, mean, std, out_w, out_b, out):
             nc.scalar.activation(out=nm_u[u][:, j, :], in_=x_t[0][:, j, cols(u)], func=ACT.Identity,
                                  scale=-1.0, bias=mu_ap[(0, j)])
 
-        def centre_gpsimd(j, lo, hi):
-            nc.gpsimd.tensor_scalar(out=nm0[:, j, lo:hi], in0=x_t[0][:, j, lo:hi], scalar1=-1.0,
+        def centre_row_gpsimd(j):
+            nc.gpsimd.tensor_scalar(out=nm0[:, j, :], in0=x_t[0][:, j, :], scalar1=-1.0,
                                     scalar2=mu_ap[(0, j)], op0=ALU.mult, op1=ALU.add)
 
         def minus_norm_rows(u, rows):
@@ -229,7 +234,7 @@ def tile_aattn_pb_t_kernel(tc, content, mean, std, out_w, out_b, out):
             for h in range(2):
                 st = psum.tile([P, 2, VC[u]], F32, name="st", tag="bank")
                 for r in range(2):
-                    nc.tensor.matmul(out=st[:, r, :], lhsT=ident_bf[:], rhs=s_t[b][:, 2 * h + r, c0:c0 + VC[u]],
+                    nc.tensor.matmul(out=st[:, r, :], lhsT=ident_bf[:], rhs=std_of(u)[:, 2 * h + r, 0:VC[u]],
                                      start=True, stop=True)
                 st_u[u].append(st)
 
@@ -241,10 +246,10 @@ def tile_aattn_pb_t_kernel(tc, content, mean, std, out_w, out_b, out):
             c0 = (u % 2) * HALF
             if g:
                 nc.gpsimd.tensor_tensor(out=pr[:, J - g:J, :], in0=nm_u[u][:, J - g:J, :],
-                                        in1=s_t[b][:, J - g:J, cols(u)], op=ALU.mult)
+                                        in1=std_of(u)[:, J - g:J, :], op=ALU.mult)
             if VC[u]:
                 nc.gpsimd.tensor_tensor(out=pr[:, :, VC[u]:HALF], in0=nm_u[u][:, :, VC[u]:HALF],
-                                        in1=s_t[b][:, :, c0 + VC[u]:c0 + HALF], op=ALU.mult)
+                                        in1=std_of(u)[:, :, VC[u]:HALF], op=ALU.mult)
 
         def prod_vector(u):
             b = u // 2
@@ -253,7 +258,7 @@ def tile_aattn_pb_t_kernel(tc, content, mean, std, out_w, out_b, out):
             if b == 0:
                 for j in ((1, 0, 2, 3) if v == J else range(v)):
                     nc.vector.scalar_tensor_tensor(out=pr[:, j, :], in0=nm_u[u][:, j, :], scalar=rstd_ap[(0, j)],
-                                                   in1=s_t[0][:, j, cols(u)], op0=ALU.mult, op1=ALU.mult)
+                                                   in1=std_of(u)[:, j, :], op0=ALU.mult, op1=ALU.mult)
             else:
                 for h in range(2):
                     nc.vector.tensor_tensor(out=pr[:, 2 * h:2 * h + 2, 0:VC[u]], in0=nm_u[u][:, 2 * h:2 * h + 2, 0:VC[u]],
@@ -265,7 +270,7 @@ def tile_aattn_pb_t_kernel(tc, content, mean, std, out_w, out_b, out):
             og_u[u] = og
             nc.vector.tensor_tensor(
                 out=og[:].rearrange("p (c i t) -> p c t i", i=RUN, t=J),
-                in0=m_t[b][:, :, cols(u)].rearrange("p t (c i) -> p c t i", i=RUN),
+                in0=mean_of(u).rearrange("p t (c i) -> p c t i", i=RUN),
                 in1=pr_u[u][:].rearrange("p t (c i) -> p c t i", i=RUN),
                 op=(ALU.subtract if b == 0 else ALU.add))
 
@@ -299,8 +304,8 @@ def tile_aattn_pb_t_kernel(tc, content, mean, std, out_w, out_b, out):
         def exit_bank(u, j, store):
             b = u // 2
             ot = exit_tile(u)
-            nc.vector.scalar_tensor_tensor(out=ot[:, j, :], in0=ac_u[u][j][:], scalar=b_f[:, j:j + 1],
-                                           in1=x_t[b][:, j, cols(u)], op0=ALU.add, op1=ALU.add)
+            nc.vector.scalar_tensor_tensor(out=ot[:, j, :], in0=x_t[b][:, j, cols(u)], scalar=b_f[:, j:j + 1],
+                                           in1=ac_u[u][j][:], op0=ALU.add, op1=ALU.add)
             if store:
                 nc.sync.dma_start(out=ov[b][:, j:j + 1, cols(u)], in_=ot[:, j:j + 1, :])
 
@@ -370,10 +375,8 @@ def tile_aattn_pb_t_kernel(tc, content, mean, std, out_w, out_b, out):
         sums_scalar(0, range(NS[0]))
         squares_scalar(0)
         stats_vector(0)
-        for j, lo, hi in G_CENTRE:
-            centre_gpsimd(j, lo, hi)
-        for u, j in S_CENTRE_A:
-            centre_row(u, j)
+        centre_row_gpsimd(1)
+        centre_row_gpsimd(0)
         sqrt_vector_rows(0)
         centre_row(0, 2)
         centre_row(0, 3)
@@ -381,8 +384,6 @@ def tile_aattn_pb_t_kernel(tc, content, mean, std, out_w, out_b, out):
         prod_gpsimd(0)
         prod_vector(0)
         minus_norm_rows(1, [2, 3])
-        for u, j in S_CENTRE_B:
-            centre_row(u, j)
         add_regroup(0)
         prod_gpsimd(1)
         hook("start")

@@ -23,7 +23,7 @@ FLOPS = 2 * C * C * B * NPIX
 
 NS = [1, 2, 3, 3]
 GP = [0, 2, 0, 0, 0, 0, 0, 0]
-VC = [0, 0, 96, 192, 96, 192, 192, 192]
+VC = [0, 0, 128, 224, 128, 224, 224, 224]
 BN_AT = {1: "start", 2: (0, "c"), 3: (2, "c")}
 RECIP_AT = {1: (0, "a"), 2: (2, "a"), 3: (4, "b")}
 FILL = [0, 0, 0, 0]

@@ -21,9 +21,9 @@ UNITS = 2 * B
 EPS = 1e-5
 FLOPS = 2 * C * C * B * NPIX
 
-NS = [1, 2, 3, 3]
+NS = [1, 2, 3, 4]
 GP = [0, 2, 0, 0, 0, 0, 0, 0]
-VC = [0, 0, 128, 224, 128, 224, 224, 224]
+VC = [0, 0, 128, 224, 224, 224, 224, 224]
 BN_AT = {1: "start", 2: (0, "c"), 3: (2, "c")}
 RECIP_AT = {1: (0, "a"), 2: (2, "a"), 3: (4, "b")}
 FILL = [0, 0, 0, 0]
@@ -59,7 +59,7 @@ def tile_aattn_pb_t_kernel(tc, content, mean, std, out_w, out_b, out):
         warm_t = keep.tile([P, 1], F32, name="warm_t")
         nc.vector.memset(one_t[:], 1.0)
         nc.vector.memset(eps_t[:], EPS)
-        nc.scalar.activation(out=warm_t[:], in_=one_t[:], func=ACT.Sqrt)
+        nc.scalar.activation(out=warm_t[:], in_=one_t[:], func=ACT.Abs_reciprocal_sqrt)
         ident = keep.tile([P, P], F32, name="ident")
         make_identity(nc, ident[:])
         ident_bf = keep.tile([P, P], BF16, name="ident_bf")
@@ -100,7 +100,6 @@ def tile_aattn_pb_t_kernel(tc, content, mean, std, out_w, out_b, out):
         mu_ap = {}
         rstd_ap = {}
         nbias_ap = {}
-        sd_t = [keep.tile([P, 2, J], F32, name="sd%d" % b) for b in range(B)]
         rs_t = [keep.tile([P, 2, J], F32, name="rs%d" % b) for b in range(B)]
         nb_t = [keep.tile([P, J], F32, name="nb%d" % b) for b in range(B)]
         ag_t = {}
@@ -124,7 +123,7 @@ def tile_aattn_pb_t_kernel(tc, content, mean, std, out_w, out_b, out):
                 nc.scalar.activation(out=junk[:], in_=x_t[b][:, j, :], func=ACT.Square,
                                      scale=-float(NPIX), bias=sm_t[b][:, j:j + 1], accum_out=sq[:, j:j + 1])
                 mu_ap[(b, j)] = mu[:, j:j + 1] if b == 0 else sm_t[b][:, j:j + 1]
-            nc.scalar.activation(out=sd_t[b][:, 0, 0:n], in_=sq[:], func=ACT.Sqrt,
+            nc.scalar.activation(out=rs_t[b][:, 0, 0:n], in_=sq[:], func=ACT.Abs_reciprocal_sqrt,
                                  scale=1.0 / (float(NPIX) * NPIX * (NPIX - 1)), bias=eps_t[:, 0:1])
 
         def aggregate(b, k):
@@ -153,20 +152,16 @@ def tile_aattn_pb_t_kernel(tc, content, mean, std, out_w, out_b, out):
 
         def sqrt_vector_rows(b):
             if b in ag_t:
-                nc.scalar.activation(out=sd_t[b][:, 0, NS[b]:J], in_=ag_t[b][:, :, 1], func=ACT.Sqrt,
+                nc.scalar.activation(out=rs_t[b][:, 0, NS[b]:J], in_=ag_t[b][:, :, 1], func=ACT.Abs_reciprocal_sqrt,
                                      scale=float(NPIX) / (NPIX - 1), bias=eps_t[:, 0:1])
 
         def negate_sd(b):
             n = NS[b]
-            nc.scalar.mul(out=sd_t[b][:, 1, 0:n], in_=sd_t[b][:, 0, 0:n], mul=-float(NPIX))
+            nc.scalar.mul(out=rs_t[b][:, 1, 0:n], in_=rs_t[b][:, 0, 0:n], mul=-1.0 / NPIX)
             if n < J:
-                nc.scalar.mul(out=sd_t[b][:, 1, n:J], in_=sd_t[b][:, 0, n:J], mul=-1.0)
+                nc.scalar.mul(out=rs_t[b][:, 1, n:J], in_=rs_t[b][:, 0, n:J], mul=-1.0)
 
         def reciprocal(b, both=True):
-            if both:
-                nc.vector.reciprocal(out=rs_t[b][:], in_=sd_t[b][:])
-            else:
-                nc.vector.reciprocal(out=rs_t[b][:, 0, :], in_=sd_t[b][:, 0, :])
             for j in range(J):
                 rstd_ap[(b, j)] = rs_t[b][:, 0, j:j + 1]
 

@@ -27,7 +27,7 @@ VC = [0, 0, 128, 224, 224, 224, 224, 224]
 BN_AT = {1: "start", 2: (0, "c"), 3: (2, "c")}
 RECIP_AT = {1: (0, "a"), 2: (2, "a"), 3: (4, "b")}
 FILL = [0, 0, 0, 0]
-RUN = 4
+RUN = 8
 TAIL_SPLIT = True
 EARLY6 = 0
 HEAD_G = True

@@ -78,8 +78,8 @@ def tile_aattn_pb_t_kernel(tc, content, mean, std, out_w, out_b, out):
             return m0_h[u][:] if u < 2 else m_t[u // 2][:, :, (u % 2) * HALF:(u % 2 + 1) * HALF]
         w_sb = keep.tile([P, J, C], BF16, name="w_sb")
         b_bf = keep.tile([P, J], BF16, name="b_bf")
-        for j in (1, 0, 2, 3):
-            nc.sync.dma_start(out=x_t[0][:, j, :], in_=xv[0][:, j, :])
+        for j, h in ((1, 0), (1, 1), (0, 0), (2, 0), (0, 1), (2, 1), (3, 0), (3, 1)):
+            nc.sync.dma_start(out=x_t[0][:, j, h * HALF:(h + 1) * HALF], in_=xv[0][:, j, h * HALF:(h + 1) * HALF])
         nc.sync.dma_start(out=s0_h[0][:], in_=sv[0][:, :, 0:HALF])
         nc.sync.dma_start(out=x_t[1][:, 0:2, :], in_=xv[1][:, 0:2, :])
         nc.sync.dma_start(out=m0_h[0][:], in_=mv[0][:, :, 0:HALF])
@@ -125,6 +125,26 @@ def tile_aattn_pb_t_kernel(tc, content, mean, std, out_w, out_b, out):
                 mu_ap[(b, j)] = mu[:, j:j + 1] if b == 0 else sm_t[b][:, j:j + 1]
             nc.scalar.activation(out=rs_t[b][:, 0, 0:n], in_=sq[:], func=ACT.Abs_reciprocal_sqrt,
                                  scale=1.0 / (float(NPIX) * NPIX * (NPIX - 1)), bias=eps_t[:, 0:1])
+
+        def stats_scalar_first():
+            smh = keep.tile([P, 2], F32, name="smh")
+            mu = keep.tile([P, 1], F32, name="mus0")
+            sq = keep.tile([P, 1], F32, name="sq0")
+            for h in range(2):
+                junk = junkp.tile([P, NPIX], BF16, name="junk")
+                nc.scalar.activation(out=junk[:, 0:HALF], in_=x_t[0][:, 0, h * HALF:(h + 1) * HALF], func=ACT.Identity,
+                                     scale=1.0 / NPIX, accum_out=smh[:, h:h + 1])
+            nc.scalar.activation(out=mu[:], in_=smh[:, 0:1], func=ACT.Identity, bias=smh[:, 1:2])
+            junk = junkp.tile([P, NPIX], BF16, name="junk")
+            nc.scalar.activation(out=junk[:], in_=x_t[0][:, 0, :], func=ACT.Square, scale=-1.0, bias=mu[:, 0:1],
+                                 accum_out=sq[:, 0:1])
+            mu_ap[(0, 0)] = mu[:, 0:1]
+            nc.scalar.activation(out=rs_t[0][:, 0, 0:1], in_=sq[:], func=ACT.Abs_reciprocal_sqrt,
+                                 scale=1.0 / (NPIX - 1), bias=eps_t[:, 0:1])
+
+        def rstd_vector_rows(b, k0, k1):
+            nc.scalar.activation(out=rs_t[b][:, 0, NS[b] + k0:NS[b] + k1], in_=ag_t[b][:, k0:k1, 1],
+                                 func=ACT.Abs_reciprocal_sqrt, scale=float(NPIX) / (NPIX - 1), bias=eps_t[:, 0:1])
 
         def aggregate(b, k):
             st, ag = st_t[b]
@@ -251,7 +271,7 @@ def tile_aattn_pb_t_kernel(tc, content, mean, std, out_w, out_b, out):
             pr = pr_u[u]
             v = J - GP[u]
             if b == 0:
-                for j in ((1, 0, 2, 3) if v == J else range(v)):
+                for j in ((1, 2, 0, 3) if v == J else range(v)):
                     nc.vector.scalar_tensor_tensor(out=pr[:, j, :], in0=nm_u[u][:, j, :], scalar=rstd_ap[(0, j)],
                                                    in1=std_of(u)[:, j, :], op0=ALU.mult, op1=ALU.mult)
             else:
@@ -367,13 +387,13 @@ def tile_aattn_pb_t_kernel(tc, content, mean, std, out_w, out_b, out):
                     norm(2 * b)
                     norm(2 * b + 1)
 
-        sums_scalar(0, range(NS[0]))
-        squares_scalar(0)
+        stats_scalar_first()
         stats_vector(0)
         centre_row_gpsimd(1)
         centre_row_gpsimd(0)
-        sqrt_vector_rows(0)
+        rstd_vector_rows(0, 0, 2)
         centre_row(0, 2)
+        rstd_vector_rows(0, 2, 3)
         centre_row(0, 3)
         reciprocal(0, both=False)
         prod_gpsimd(0)

@@ -324,6 +324,14 @@ def tile_aattn_pb_t_kernel(tc, content, mean, std, out_w, out_b, out):
             if store:
                 nc.sync.dma_start(out=ov[b][:, j:j + 1, cols(u)], in_=ot[:, j:j + 1, :])
 
+        def exit_part(u, j, lo, hi):
+            b = u // 2
+            ot = exit_tile(u)
+            c0 = (u % 2) * HALF
+            nc.vector.scalar_tensor_tensor(out=ot[:, j, lo:hi], in0=x_t[b][:, j, c0 + lo:c0 + hi], scalar=b_f[:, j:j + 1],
+                                           in1=ac_u[u][j][:, lo:hi], op0=ALU.add, op1=ALU.add)
+            nc.sync.dma_start(out=ov[b][:, j:j + 1, c0 + lo:c0 + hi], in_=ot[:, j:j + 1, lo:hi])
+
         def exit_bank_helped(u):
             b = u // 2
             ot = exit_tile(u)
@@ -402,41 +410,37 @@ def tile_aattn_pb_t_kernel(tc, content, mean, std, out_w, out_b, out):
         add_regroup(0)
         prod_gpsimd(1)
         hook("start")
-        for u in range(UNITS):
+        for u in range(UNITS - 2):
             nxt = u + 1
-            if nxt < UNITS:
-                prod_vector(nxt)
+            prod_vector(nxt)
             for b in range(B):
                 if late_aggr.get(b):
                     aggregate(b, 0)
                     late_aggr[b] = False
             hook((u, "a"))
-            if u not in cd_u:
-                quantise(u)
-                if u == 0:
-                    weights_quantise()
-                    nc.vector.tensor_copy(out=b_f[:], in_=b_bf[:])
-                multiply(u)
-            if u + 2 < UNITS:
-                stage_std(u + 2)
+            quantise(u)
+            if u == 0:
+                weights_quantise()
+                nc.vector.tensor_copy(out=b_f[:], in_=b_bf[:])
+            multiply(u)
+            stage_std(u + 2)
             hook((u, "b"))
-            if u == UNITS - 2:
-                for j in range(EARLY6):
-                    exit_bank(u, j, True)
-            if nxt < UNITS:
-                add_regroup(nxt)
-            if nxt + 1 < UNITS:
-                prod_gpsimd(nxt + 1)
-            if nxt == UNITS - 1:
-                quantise(nxt)
-                multiply(nxt)
-            if u < UNITS - 2:
-                finish(u)
-            else:
-                if TAIL_G:
-                    exit_bank_helped(u)
-                for j in range(EARLY6 if u == UNITS - 2 else 0, 3 if TAIL_G else J):
-                    exit_bank(u, j, True)
-                if TAIL_G:
-                    nc.sync.dma_start(out=ov[u // 2][:, 3:4, cols(u)], in_=ot_u[u][:, 3:4, :])
+            add_regroup(nxt)
+            prod_gpsimd(nxt + 1)
+            finish(u)
             hook((u, "c"))
+
+        prod_vector(7)
+        quantise(6)
+        multiply(6)
+        add_regroup(7)
+        exit_bank(6, 0, True)
+        exit_bank(6, 1, True)
+        quantise(7)
+        multiply(7)
+        exit_bank(6, 2, True)
+        exit_bank(6, 3, True)
+        for j in range(J - 1):
+            exit_bank(7, j, True)
+        exit_part(7, J - 1, 0, HALF // 2)
+        exit_part(7, J - 1, HALF // 2, HALF)

@@ -263,8 +263,9 @@ def tile_aattn_pb_t_kernel(tc, content, mean, std, out_w, out_b, out):
                 nc.gpsimd.tensor_tensor(out=pr[:, J - g:J, :], in0=nm_u[u][:, J - g:J, :],
                                         in1=std_of(u)[:, J - g:J, :], op=ALU.mult)
             if VC[u]:
-                nc.gpsimd.tensor_tensor(out=pr[:, :, VC[u]:HALF], in0=nm_u[u][:, :, VC[u]:HALF],
-                                        in1=std_of(u)[:, :, VC[u]:HALF], op=ALU.mult)
+                for lo, hi in (((0, 2), (2, J)) if u == 6 else ((0, J),)):
+                    nc.gpsimd.tensor_tensor(out=pr[:, lo:hi, VC[u]:HALF], in0=nm_u[u][:, lo:hi, VC[u]:HALF],
+                                            in1=std_of(u)[:, lo:hi, VC[u]:HALF], op=ALU.mult)
 
         def prod_vector(u):
             b = u // 2

@@ -253,6 +253,13 @@ def tile_aattn_pb_t_kernel(tc, content, mean, std, out_w, out_b, out):
                                      start=True, stop=True)
                 st_u[u].append(st)
 
+        def stage_std_rows(u, rows):
+            st_u[u] = {}
+            for j in rows:
+                st = psum.tile([P, HALF], F32, name="st", tag="bank")
+                nc.tensor.matmul(out=st[:], lhsT=ident_bf[:], rhs=std_of(u)[:, j, :], start=True, stop=True)
+                st_u[u][j] = st
+
         def prod_gpsimd(u):
             b = u // 2
             pr = mp.tile([P, J, HALF], F32, name="pr")
@@ -274,7 +281,8 @@ def tile_aattn_pb_t_kernel(tc, content, mean, std, out_w, out_b, out):
             if b == 0:
                 for j in ((1, 2, 0, 3) if v == J else range(v)):
                     nc.vector.scalar_tensor_tensor(out=pr[:, j, :], in0=nm_u[u][:, j, :], scalar=rstd_ap[(0, j)],
-                                                   in1=std_of(u)[:, j, :], op0=ALU.mult, op1=ALU.mult)
+                                                   in1=st_u[u][j][:] if u in st_u else std_of(u)[:, j, :],
+                                                   op0=ALU.mult, op1=ALU.mult)
             else:
                 for h in range(2):
                     nc.vector.tensor_tensor(out=pr[:, 2 * h:2 * h + 2, 0:VC[u]], in0=nm_u[u][:, 2 * h:2 * h + 2, 0:VC[u]],
@@ -410,6 +418,7 @@ def tile_aattn_pb_t_kernel(tc, content, mean, std, out_w, out_b, out):
         minus_norm_rows(1, [2, 3])
         add_regroup(0)
         prod_gpsimd(1)
+        stage_std_rows(1, (0, 1))
         hook("start")
         for u in range(UNITS - 2):
             nxt = u + 1

@@ -22,16 +22,9 @@ EPS = 1e-5
 FLOPS = 2 * C * C * B * NPIX
 
 NS = [1, 2, 3, 4]
-GP = [0, 2, 0, 0, 0, 0, 0, 0]
 VC = [0, 0, 128, 224, 224, 224, 224, 224]
-BN_AT = {1: "start", 2: (0, "c"), 3: (2, "c")}
-RECIP_AT = {1: (0, "a"), 2: (2, "a"), 3: (4, "b")}
-FILL = [0, 0, 0, 0]
 RUN = 8
-TAIL_SPLIT = True
-EARLY6 = 0
-HEAD_G = True
-TAIL_G = False
+STAGED0 = (0, 2, 3)
 
 
 def tile_aattn_pb_t_kernel(tc, content, mean, std, out_w, out_b, out):
@@ -57,27 +50,32 @@ def tile_aattn_pb_t_kernel(tc, content, mean, std, out_w, out_b, out):
         eps_t = keep.tile([P, 1], F32, name="eps_t")
         one_t = keep.tile([P, 1], F32, name="one_t")
         warm_t = keep.tile([P, 1], F32, name="warm_t")
+        minus_t = keep.tile([P, 1], F32, name="minus_t")
         nc.vector.memset(one_t[:], 1.0)
         nc.vector.memset(eps_t[:], EPS)
         nc.scalar.activation(out=warm_t[:], in_=one_t[:], func=ACT.Abs_reciprocal_sqrt)
-        ident = keep.tile([P, P], F32, name="ident")
-        make_identity(nc, ident[:])
         ident_bf = keep.tile([P, P], BF16, name="ident_bf")
         make_identity(nc, ident_bf[:])
+        ident = keep.tile([P, P], F32, name="ident")
+        make_identity(nc, ident[:])
 
         x_t = [keep.tile([P, J, NPIX], BF16, name="x%d" % b) for b in range(B)]
         s_t = [None] + [keep.tile([P, J, NPIX], BF16, name="s%d" % b) for b in range(1, B)]
         m_t = [None] + [keep.tile([P, J, NPIX], BF16, name="m%d" % b) for b in range(1, B)]
         s0_h = [keep.tile([P, J, HALF], BF16, name="s0h%d" % h) for h in range(2)]
         m0_h = [keep.tile([P, J, HALF], BF16, name="m0h%d" % h) for h in range(2)]
-
-        def std_of(u):
-            return s0_h[u][:] if u < 2 else s_t[u // 2][:, :, (u % 2) * HALF:(u % 2 + 1) * HALF]
-
-        def mean_of(u):
-            return m0_h[u][:] if u < 2 else m_t[u // 2][:, :, (u % 2) * HALF:(u % 2 + 1) * HALF]
         w_sb = keep.tile([P, J, C], BF16, name="w_sb")
         b_bf = keep.tile([P, J], BF16, name="b_bf")
+
+        def cols(u):
+            return slice((u % 2) * HALF, (u % 2 + 1) * HALF)
+
+        def std_of(u):
+            return s0_h[u][:] if u < 2 else s_t[u // 2][:, :, cols(u)]
+
+        def mean_of(u):
+            return m0_h[u][:] if u < 2 else m_t[u // 2][:, :, cols(u)]
+
         for j, h in ((1, 0), (1, 1), (0, 0), (2, 0), (0, 1), (2, 1), (3, 0), (3, 1)):
             nc.sync.dma_start(out=x_t[0][:, j, h * HALF:(h + 1) * HALF], in_=xv[0][:, j, h * HALF:(h + 1) * HALF])
         nc.sync.dma_start(out=s0_h[0][:], in_=sv[0][:, :, 0:HALF])
@@ -89,162 +87,103 @@ def tile_aattn_pb_t_kernel(tc, content, mean, std, out_w, out_b, out):
         nc.sync.dma_start(out=m0_h[1][:], in_=mv[0][:, :, HALF:NPIX])
         nc.sync.dma_start(out=b_bf[:], in_=bv)
         nc.sync.dma_start(out=s_t[1][:], in_=sv[1])
+        nc.sync.dma_start(out=x_t[2][:], in_=xv[2])
         nc.sync.dma_start(out=m_t[1][:], in_=mv[1])
-        for b in range(2, B):
-            nc.sync.dma_start(out=x_t[b][:], in_=xv[b])
-            nc.sync.dma_start(out=s_t[b][:], in_=sv[b])
-            nc.sync.dma_start(out=m_t[b][:], in_=mv[b])
+        nc.sync.dma_start(out=s_t[2][:], in_=sv[2])
+        nc.sync.dma_start(out=x_t[3][:], in_=xv[3])
+        nc.sync.dma_start(out=m_t[2][:], in_=mv[2])
+        nc.sync.dma_start(out=s_t[3][:], in_=sv[3])
+        nc.sync.dma_start(out=m_t[3][:], in_=mv[3])
 
-        b_f = keep.tile([P, J], F32, name="b_f")
+        rstd = [keep.tile([P, J], F32, name="rstd%d" % b) for b in range(B)]
+        nbias = [keep.tile([P, J], F32, name="nbias%d" % b) for b in range(B)]
+        nrstd = [keep.tile([P, J], F32, name="nrstd%d" % b) for b in range(B)]
+        nmean = [keep.tile([P, J], F32, name="nmean%d" % b) for b in range(B)]
+        ssq = [keep.tile([P, J], F32, name="ssq%d" % b) for b in range(B)]
+        st_t = [keep.tile([P, J, 2, 6], F32, name="st%d" % b) for b in range(B)]
+        ag_t = [keep.tile([P, J, 2], F32, name="ag%d" % b) for b in range(B)]
 
-        mu_ap = {}
-        rstd_ap = {}
-        nbias_ap = {}
-        rs_t = [keep.tile([P, 2, J], F32, name="rs%d" % b) for b in range(B)]
-        nb_t = [keep.tile([P, J], F32, name="nb%d" % b) for b in range(B)]
-        ag_t = {}
-
-        def sums_scalar(b, rows):
-            if b not in sm_t:
-                sm_t[b] = keep.tile([P, NS[b]], F32, name="sm%d" % b)
-            for j in rows:
-                junk = junkp.tile([P, NPIX], BF16, name="junk")
-                nc.scalar.activation(out=junk[:], in_=x_t[b][:, j, :], func=ACT.Identity,
-                                     accum_out=sm_t[b][:, j:j + 1])
-
-        def squares_scalar(b):
-            n = NS[b]
-            sq = keep.tile([P, n], F32, name="sq%d" % b)
-            if b == 0:
-                mu = keep.tile([P, n], F32, name="mus%d" % b)
-                nc.scalar.mul(out=mu[:], in_=sm_t[b][:], mul=1.0 / NPIX)
-            for j in range(n):
-                junk = junkp.tile([P, NPIX], BF16, name="junk")
-                nc.scalar.activation(out=junk[:], in_=x_t[b][:, j, :], func=ACT.Square,
-                                     scale=-float(NPIX), bias=sm_t[b][:, j:j + 1], accum_out=sq[:, j:j + 1])
-                mu_ap[(b, j)] = mu[:, j:j + 1] if b == 0 else sm_t[b][:, j:j + 1]
-            nc.scalar.activation(out=rs_t[b][:, 0, 0:n], in_=sq[:], func=ACT.Abs_reciprocal_sqrt,
-                                 scale=1.0 / (float(NPIX) * NPIX * (NPIX - 1)), bias=eps_t[:, 0:1])
-
-        def stats_scalar_first():
-            smh = keep.tile([P, 2], F32, name="smh")
-            mu = keep.tile([P, 1], F32, name="mus0")
-            sq = keep.tile([P, 1], F32, name="sq0")
-            for h in range(2):
-                junk = junkp.tile([P, NPIX], BF16, name="junk")
-                nc.scalar.activation(out=junk[:, 0:HALF], in_=x_t[0][:, 0, h * HALF:(h + 1) * HALF], func=ACT.Identity,
-                                     scale=1.0 / NPIX, accum_out=smh[:, h:h + 1])
-            nc.scalar.activation(out=mu[:], in_=smh[:, 0:1], func=ACT.Identity, bias=smh[:, 1:2])
+        def sum_scalar(b, j):
             junk = junkp.tile([P, NPIX], BF16, name="junk")
-            nc.scalar.activation(out=junk[:], in_=x_t[0][:, 0, :], func=ACT.Square, scale=-1.0, bias=mu[:, 0:1],
-                                 accum_out=sq[:, 0:1])
-            mu_ap[(0, 0)] = mu[:, 0:1]
-            nc.scalar.activation(out=rs_t[0][:, 0, 0:1], in_=sq[:], func=ACT.Abs_reciprocal_sqrt,
+            nc.scalar.activation(out=junk[:], in_=x_t[b][:, j, :], func=ACT.Identity, scale=-1.0 / NPIX,
+                                 accum_out=nmean[b][:, j:j + 1])
+
+        def square_scalar(b, j):
+            junk = junkp.tile([P, NPIX], BF16, name="junk")
+            nc.scalar.activation(out=junk[:], in_=x_t[b][:, j, :], func=ACT.Square, bias=nmean[b][:, j:j + 1],
+                                 accum_out=ssq[b][:, j:j + 1])
+
+        def rstd_scalar(b, lo, hi):
+            nc.scalar.activation(out=rstd[b][:, lo:hi], in_=ssq[b][:, lo:hi], func=ACT.Abs_reciprocal_sqrt,
                                  scale=1.0 / (NPIX - 1), bias=eps_t[:, 0:1])
 
-        def rstd_vector_rows(b, k0, k1):
-            nc.scalar.activation(out=rs_t[b][:, 0, NS[b] + k0:NS[b] + k1], in_=ag_t[b][:, k0:k1, 1],
-                                 func=ACT.Abs_reciprocal_sqrt, scale=float(NPIX) / (NPIX - 1), bias=eps_t[:, 0:1])
+        def rstd_vector(b, lo, hi):
+            nc.scalar.activation(out=rstd[b][:, lo:hi], in_=ag_t[b][:, lo:hi, 1], func=ACT.Abs_reciprocal_sqrt,
+                                 scale=float(NPIX) / (NPIX - 1), bias=eps_t[:, 0:1])
 
-        def aggregate(b, k):
-            st, ag = st_t[b]
-            nc.vector.bn_aggr(out=ag[:, k, :], in_=st[:, k, :, :].rearrange("p c s -> p (c s)"))
+        def negate_rstd(b, lo, hi):
+            nc.scalar.mul(out=nrstd[b][:, lo:hi], in_=rstd[b][:, lo:hi], mul=-1.0)
 
-        def stats_vector(b):
-            n = J - NS[b]
-            if n == 0:
-                return
-            st = keep.tile([P, n, 2, 6], F32, name="st%d" % b)
-            ag = keep.tile([P, n, 2], F32, name="ag%d" % b)
-            ag_t[b] = ag
-            st_t[b] = (st, ag)
-            for k in range(n):
-                j = NS[b] + k
-                for c in range(2):
-                    nc.vector.bn_stats(out=st[:, k, c, :], in_=x_t[b][:, j, c * HALF:(c + 1) * HALF])
-                    if c == 0 and k > 0:
-                        aggregate(b, k - 1)
-                mu_ap[(b, j)] = ag[:, k, 0:1]
-            if n > 1:
-                aggregate(b, n - 1)
+        def nbias_row(b, j):
+            if j < NS[b]:
+                nc.scalar.activation(out=nbias[b][:, j:j + 1], in_=nmean[b][:, j:j + 1], func=ACT.Identity,
+                                     scale=rstd[b][:, j:j + 1])
             else:
-                late_aggr[b] = True
+                nc.scalar.activation(out=nbias[b][:, j:j + 1], in_=ag_t[b][:, j, 0:1], func=ACT.Identity,
+                                     scale=nrstd[b][:, j:j + 1])
 
-        def sqrt_vector_rows(b):
-            if b in ag_t:
-                nc.scalar.activation(out=rs_t[b][:, 0, NS[b]:J], in_=ag_t[b][:, :, 1], func=ACT.Abs_reciprocal_sqrt,
-                                     scale=float(NPIX) / (NPIX - 1), bias=eps_t[:, 0:1])
+        def bn(b, j, h):
+            nc.vector.bn_stats(out=st_t[b][:, j, h, :], in_=x_t[b][:, j, h * HALF:(h + 1) * HALF])
 
-        def negate_sd(b):
-            n = NS[b]
-            nc.scalar.mul(out=rs_t[b][:, 1, 0:n], in_=rs_t[b][:, 0, 0:n], mul=-1.0 / NPIX)
-            if n < J:
-                nc.scalar.mul(out=rs_t[b][:, 1, n:J], in_=rs_t[b][:, 0, n:J], mul=-1.0)
-
-        def reciprocal(b, both=True):
-            for j in range(J):
-                rstd_ap[(b, j)] = rs_t[b][:, 0, j:j + 1]
-
-        def biases(b):
-            for j in range(J):
-                nc.scalar.activation(out=nb_t[b][:, j:j + 1], in_=mu_ap[(b, j)], func=ACT.Identity,
-                                     scale=rs_t[b][:, 1, j:j + 1])
-                nbias_ap[(b, j)] = nb_t[b][:, j:j + 1]
-
-        sm_t = {}
-        st_t = {}
-        late_aggr = {}
+        def aggregate(b, j):
+            nc.vector.bn_aggr(out=ag_t[b][:, j, :], in_=st_t[b][:, j, :, :].rearrange("p c s -> p (c s)"))
 
         nm_u = {}
         pr_u = {}
         og_u = {}
         cd_u = {}
         ac_u = {}
-
-        def cols(u):
-            h = u % 2
-            return slice(h * HALF, (h + 1) * HALF)
+        st_u = {}
+        ot_u = {}
 
         nm0 = keep.tile([P, J, NPIX], F32, name="nm0")
         nm_u[0] = nm0[:, :, 0:HALF]
         nm_u[1] = nm0[:, :, HALF:NPIX]
+        mu0 = keep.tile([P, 1], F32, name="mu0")
 
-        def centre_row(u, j):
+        def mean0(j):
+            return mu0[:, 0:1] if j == 0 else ag_t[0][:, j, 0:1]
+
+        def centre_scalar(u, j):
             nc.scalar.activation(out=nm_u[u][:, j, :], in_=x_t[0][:, j, cols(u)], func=ACT.Identity,
-                                 scale=-1.0, bias=mu_ap[(0, j)])
+                                 scale=-1.0, bias=mean0(j))
 
-        def centre_row_gpsimd(j):
-            nc.gpsimd.tensor_scalar(out=nm0[:, j, :], in0=x_t[0][:, j, :], scalar1=-1.0,
-                                    scalar2=mu_ap[(0, j)], op0=ALU.mult, op1=ALU.add)
+        def centre_gpsimd(u, j):
+            nc.gpsimd.tensor_scalar(out=nm_u[u][:, j, :], in0=x_t[0][:, j, cols(u)],
+                                    scalar1=(-1.0 if u == 0 else minus_t[:, 0:1]),
+                                    scalar2=mean0(j), op0=ALU.mult, op1=ALU.add)
 
-        def minus_norm_rows(u, rows):
-            lo = rows[0]
-            hi = rows[-1] + 1
-            nrs = keep.tile([P, J], F32, name="nrs0")
-            pb = keep.tile([P, J], F32, name="pb0")
-            nc.scalar.mul(out=nrs[:, lo:hi], in_=rs_t[0][:, 0, lo:hi], mul=-1.0)
+        def minus_norm(u, rows):
+            lo, hi = rows[0], rows[-1] + 1
+            negate_rstd(0, lo, hi)
             for j in rows:
-                nc.scalar.activation(out=pb[:, j:j + 1], in_=mu_ap[(0, j)], func=ACT.Identity,
-                                     scale=rs_t[0][:, 0, j:j + 1])
+                nc.scalar.activation(out=nbias[0][:, j:j + 1], in_=mean0(j), func=ACT.Identity,
+                                     scale=rstd[0][:, j:j + 1])
+            sum_scalar(1, 0)
             for j in rows:
                 nc.scalar.activation(out=nm_u[u][:, j, :], in_=x_t[0][:, j, cols(u)], func=ACT.Identity,
-                                     scale=nrs[:, j:j + 1], bias=pb[:, j:j + 1])
+                                     scale=nrstd[0][:, j:j + 1], bias=nbias[0][:, j:j + 1])
 
-        def norm(u):
+        def norm_row(u, j, lo, hi):
             b = u // 2
-            nm = nmp.tile([P, J, HALF], F32, name="nm")
-            nm_u[u] = nm
             c0 = (u % 2) * HALF
-            for lo, hi in ((VC[u], HALF), (0, VC[u])):
-                for j in range(J):
-                    nc.scalar.activation(out=nm[:, j, lo:hi], in_=x_t[b][:, j, c0 + lo:c0 + hi], func=ACT.Identity,
-                                         scale=rstd_ap[(b, j)], bias=nbias_ap[(b, j)])
+            nc.scalar.activation(out=nm_u[u][:, j, lo:hi], in_=x_t[b][:, j, c0 + lo:c0 + hi], func=ACT.Identity,
+                                 scale=rstd[b][:, j:j + 1], bias=nbias[b][:, j:j + 1])
 
-        st_u = {}
+        def norm_tile(u):
+            nm_u[u] = nmp.tile([P, J, HALF], F32, name="nm")
 
         def stage_std(u):
-            b = u // 2
-            c0 = (u % 2) * HALF
             st_u[u] = []
             for h in range(2):
                 st = psum.tile([P, 2, VC[u]], F32, name="st", tag="bank")
@@ -260,43 +199,36 @@ def tile_aattn_pb_t_kernel(tc, content, mean, std, out_w, out_b, out):
                 nc.tensor.matmul(out=st[:], lhsT=ident_bf[:], rhs=std_of(u)[:, j, :], start=True, stop=True)
                 st_u[u][j] = st
 
-        def prod_gpsimd(u):
-            b = u // 2
-            pr = mp.tile([P, J, HALF], F32, name="pr")
-            pr_u[u] = pr
-            g = GP[u]
-            c0 = (u % 2) * HALF
-            if g:
-                nc.gpsimd.tensor_tensor(out=pr[:, J - g:J, :], in0=nm_u[u][:, J - g:J, :],
-                                        in1=std_of(u)[:, J - g:J, :], op=ALU.mult)
-            if VC[u]:
-                for lo, hi in (((0, 2), (2, J)) if u == 6 else ((0, J),)):
-                    nc.gpsimd.tensor_tensor(out=pr[:, lo:hi, VC[u]:HALF], in0=nm_u[u][:, lo:hi, VC[u]:HALF],
-                                            in1=std_of(u)[:, lo:hi, VC[u]:HALF], op=ALU.mult)
+        def product_tile(u):
+            pr_u[u] = mp.tile([P, J, HALF], F32, name="pr")
 
-        def prod_vector(u):
-            b = u // 2
-            pr = pr_u[u]
-            v = J - GP[u]
-            if b == 0:
-                for j in ((1, 2, 0, 3) if v == J else range(v)):
-                    nc.vector.scalar_tensor_tensor(out=pr[:, j, :], in0=nm_u[u][:, j, :], scalar=rstd_ap[(0, j)],
-                                                   in1=st_u[u][j][:] if u in st_u else std_of(u)[:, j, :],
-                                                   op0=ALU.mult, op1=ALU.mult)
-            else:
-                for h in range(2):
-                    nc.vector.tensor_tensor(out=pr[:, 2 * h:2 * h + 2, 0:VC[u]], in0=nm_u[u][:, 2 * h:2 * h + 2, 0:VC[u]],
-                                            in1=st_u[u][h][:], op=ALU.mult)
+        def product_gpsimd(u, lo, hi, c0):
+            nc.gpsimd.tensor_tensor(out=pr_u[u][:, lo:hi, c0:HALF], in0=nm_u[u][:, lo:hi, c0:HALF],
+                                    in1=std_of(u)[:, lo:hi, c0:HALF], op=ALU.mult)
+
+        def product_gpsimd_unit(u):
+            product_tile(u)
+            for lo, hi in (((0, 2), (2, J)) if u == 6 else ((0, J),)):
+                product_gpsimd(u, lo, hi, VC[u])
+
+        def product0_vector(u, j):
+            nc.vector.scalar_tensor_tensor(out=pr_u[u][:, j, :], in0=nm_u[u][:, j, :], scalar=rstd[0][:, j:j + 1],
+                                           in1=st_u[u][j][:] if j in st_u.get(u, {}) else std_of(u)[:, j, :],
+                                           op0=ALU.mult, op1=ALU.mult)
+
+        def product_vector(u):
+            for h in range(2):
+                nc.vector.tensor_tensor(out=pr_u[u][:, 2 * h:2 * h + 2, 0:VC[u]],
+                                        in0=nm_u[u][:, 2 * h:2 * h + 2, 0:VC[u]], in1=st_u[u][h][:], op=ALU.mult)
 
         def add_regroup(u):
-            b = u // 2
             og = ogp.tile([P, HALF * J], BF16, name="og", align_bytes=64)
             og_u[u] = og
             nc.vector.tensor_tensor(
                 out=og[:].rearrange("p (c i t) -> p c t i", i=RUN, t=J),
                 in0=mean_of(u).rearrange("p t (c i) -> p c t i", i=RUN),
                 in1=pr_u[u][:].rearrange("p t (c i) -> p c t i", i=RUN),
-                op=(ALU.subtract if b == 0 else ALU.add))
+                op=(ALU.subtract if u < 2 else ALU.add))
 
         def quantise(u):
             cd = cdp.tile([P, HALF], U32, name="cd", align_bytes=64)
@@ -307,7 +239,7 @@ def tile_aattn_pb_t_kernel(tc, content, mean, std, out_w, out_b, out):
         def multiply(u):
             cd, sc = cd_u[u]
             accs = {}
-            for j in ((3, 0, 1, 2) if TAIL_G and u == UNITS - 1 else range(J)):
+            for j in range(J):
                 acc = psum.tile([P, HALF], F32, name="acc", tag="bank")
                 nc.tensor.matmul_mx(out=acc[:], lhsT=w_cd[:, j * P:(j + 1) * P].bitcast(FP8X4),
                                     lhsT_scale=w_sc[:, j * P:(j + 1) * P],
@@ -316,51 +248,25 @@ def tile_aattn_pb_t_kernel(tc, content, mean, std, out_w, out_b, out):
                 accs[j] = acc
             ac_u[u] = accs
 
-        yt_box = {}
-
-        ot_u = {}
-
-        def exit_tile(u):
+        def exit_part(u, j, lo, hi, store):
+            b = u // 2
             if u not in ot_u:
                 ot_u[u] = otp.tile([P, J, HALF], F32, name="ot")
-            return ot_u[u]
-
-        def exit_bank(u, j, store):
-            b = u // 2
-            ot = exit_tile(u)
-            nc.vector.scalar_tensor_tensor(out=ot[:, j, :], in0=x_t[b][:, j, cols(u)], scalar=b_f[:, j:j + 1],
-                                           in1=ac_u[u][j][:], op0=ALU.add, op1=ALU.add)
-            if store:
-                nc.sync.dma_start(out=ov[b][:, j:j + 1, cols(u)], in_=ot[:, j:j + 1, :])
-
-        def exit_part(u, j, lo, hi):
-            b = u // 2
-            ot = exit_tile(u)
+            ot = ot_u[u]
             c0 = (u % 2) * HALF
-            nc.vector.scalar_tensor_tensor(out=ot[:, j, lo:hi], in0=x_t[b][:, j, c0 + lo:c0 + hi], scalar=b_f[:, j:j + 1],
+            nc.vector.scalar_tensor_tensor(out=ot[:, j, lo:hi], in0=x_t[b][:, j, c0 + lo:c0 + hi], scalar=b_bf[:, j:j + 1],
                                            in1=ac_u[u][j][:, lo:hi], op0=ALU.add, op1=ALU.add)
-            nc.sync.dma_start(out=ov[b][:, j:j + 1, c0 + lo:c0 + hi], in_=ot[:, j:j + 1, lo:hi])
-
-        def exit_bank_helped(u):
-            b = u // 2
-            ot = exit_tile(u)
-            if "yt" not in yt_box:
-                yt_box["yt"] = mp.tile([P, 2, HALF], F32, name="yt", tag="pr")
-            yt = yt_box["yt"]
-            k = u - (UNITS - 2)
-            nc.scalar.activation(out=yt[:, k, :], in_=ac_u[u][3][:], func=ACT.Identity, bias=b_f[:, 3:4])
-            nc.gpsimd.tensor_tensor(out=ot[:, 3, :], in0=yt[:, k, :], in1=x_t[b][:, 3, cols(u)], op=ALU.add)
+            if store:
+                nc.sync.dma_start(out=ov[b][:, j:j + 1, c0 + lo:c0 + hi], in_=ot[:, j:j + 1, lo:hi])
 
         def finish(u):
-            b = u // 2
             for j in range(J):
-                exit_bank(u, j, False)
-            nc.sync.dma_start(out=ov[b][:, :, cols(u)], in_=ot_u[u][:])
+                exit_part(u, j, 0, HALF, False)
+            nc.sync.dma_start(out=ov[u // 2][:, :, cols(u)], in_=ot_u[u][:])
 
         w_g = keep.tile([P, C * J], BF16, name="w_g", align_bytes=64)
         w_cd = keep.tile([P, C], U32, name="w_cd", align_bytes=64)
         w_sc = keep.tile([P, C], U8, name="w_sc", align_bytes=64)
-
         wt_h = []
 
         def weights_transpose():
@@ -380,77 +286,163 @@ def tile_aattn_pb_t_kernel(tc, content, mean, std, out_w, out_b, out):
         def weights_quantise():
             nc.vector.quantize_mx(out=w_cd[:].bitcast(FP8X4), scales=w_sc[:], in_=w_g[:])
 
-        def scalar_stats(b):
-            sums_scalar(b, range(FILL[b], NS[b]))
-            squares_scalar(b)
-            if b == 1:
-                weights_transpose()
-                weights_copy(0)
-            sqrt_vector_rows(b)
-            negate_sd(b)
-            if b == 1:
-                weights_copy(1)
+        def scalar_image1():
+            sum_scalar(1, 1)
+            square_scalar(1, 0)
+            square_scalar(1, 1)
+            rstd_scalar(1, 0, 1)
+            weights_transpose()
+            weights_copy(0)
+            rstd_scalar(1, 1, 2)
+            rstd_vector(1, 2, J)
+            nbias_row(1, 0)
+            weights_copy(1)
+            nbias_row(1, 1)
+            negate_rstd(1, 2, J)
+            norm_tile(2)
+            norm_row(2, 0, VC[2], HALF)
+            nbias_row(1, 2)
+            nbias_row(1, 3)
+            for j in (1, 2, 3):
+                norm_row(2, j, VC[2], HALF)
+            for j in range(J):
+                norm_row(2, j, 0, VC[2])
+            norm_tile(3)
+            for j in range(J):
+                norm_row(3, j, 0, HALF)
 
-        def hook(where):
-            for b in range(1, B):
-                if BN_AT.get(b) == where:
-                    stats_vector(b)
-                if RECIP_AT[b] == where:
-                    scalar_stats(b)
-                    if b + 1 < B:
-                        sums_scalar(b + 1, range(FILL[b + 1]))
-                    reciprocal(b)
-                    biases(b)
-                    norm(2 * b)
-                    norm(2 * b + 1)
+        def scalar_image2():
+            for j in range(3):
+                sum_scalar(2, j)
+            rstd_vector(2, 3, J)
+            square_scalar(2, 0)
+            negate_rstd(2, 3, J)
+            square_scalar(2, 1)
+            nbias_row(2, 3)
+            square_scalar(2, 2)
+            rstd_scalar(2, 0, 2)
+            norm_tile(4)
+            norm_row(4, 3, 0, HALF)
+            nbias_row(2, 0)
+            nbias_row(2, 1)
+            rstd_scalar(2, 2, 3)
+            norm_tile(5)
+            norm_row(5, 3, 0, HALF)
+            norm_row(4, 0, 0, HALF)
+            nbias_row(2, 2)
+            norm_row(4, 1, 0, HALF)
+            norm_row(4, 2, 0, HALF)
+            for j in range(3):
+                norm_row(5, j, 0, HALF)
 
-        stats_scalar_first()
-        stats_vector(0)
-        centre_row_gpsimd(1)
-        centre_row_gpsimd(0)
-        rstd_vector_rows(0, 0, 2)
-        centre_row(0, 2)
-        rstd_vector_rows(0, 2, 3)
-        centre_row(0, 3)
-        reciprocal(0, both=False)
-        prod_gpsimd(0)
-        prod_vector(0)
-        minus_norm_rows(1, [2, 3])
+        def scalar_image3():
+            for j in range(J):
+                sum_scalar(3, j)
+            square_scalar(3, 0)
+            square_scalar(3, 1)
+            rstd_scalar(3, 0, 1)
+            square_scalar(3, 2)
+            nbias_row(3, 0)
+            rstd_scalar(3, 1, 2)
+            square_scalar(3, 3)
+            nbias_row(3, 1)
+            norm_tile(6)
+            norm_row(6, 0, VC[6], HALF)
+            rstd_scalar(3, 2, J)
+            norm_row(6, 1, VC[6], HALF)
+            nbias_row(3, 2)
+            nbias_row(3, 3)
+            norm_row(6, 0, 0, VC[6])
+            norm_row(6, 2, VC[6], HALF)
+            norm_row(6, 3, VC[6], HALF)
+            for j in (1, 2, 3):
+                norm_row(6, j, 0, VC[6])
+            norm_tile(7)
+            for j in range(J):
+                norm_row(7, j, 0, HALF)
+
+        smh = keep.tile([P, 2], F32, name="smh")
+        for h in range(2):
+            junk = junkp.tile([P, NPIX], BF16, name="junk")
+            nc.scalar.activation(out=junk[:, 0:HALF], in_=x_t[0][:, 0, h * HALF:(h + 1) * HALF], func=ACT.Identity,
+                                 scale=1.0 / NPIX, accum_out=smh[:, h:h + 1])
+        product_tile(0)
+        bn(0, 1, 0)
+        bn(0, 1, 1)
+        bn(0, 2, 0)
+        aggregate(0, 1)
+        rstd_vector(0, 1, 2)
+        centre_gpsimd(0, 1)
+        nc.scalar.activation(out=mu0[:], in_=smh[:, 0:1], func=ACT.Identity, bias=smh[:, 1:2])
+        centre_gpsimd(0, 0)
+        junk = junkp.tile([P, NPIX], BF16, name="junk")
+        nc.scalar.activation(out=junk[:], in_=x_t[0][:, 0, :], func=ACT.Square, scale=-1.0, bias=mu0[:, 0:1],
+                             accum_out=ssq[0][:, 0:1])
+        bn(0, 2, 1)
+        bn(0, 3, 0)
+        aggregate(0, 2)
+        rstd_vector(0, 2, 3)
+        bn(0, 3, 1)
+        stage_std_rows(0, STAGED0)
+        product0_vector(0, 1)
+        nc.vector.memset(minus_t[:], -1.0)
+        aggregate(0, 3)
+        rstd_scalar(0, 0, 1)
+        centre_scalar(0, 2)
+        rstd_vector(0, 3, 4)
+        centre_scalar(0, 3)
+        centre_gpsimd(1, 1)
+        centre_gpsimd(1, 0)
+        product0_vector(0, 0)
+        product0_vector(0, 2)
+        product0_vector(0, 3)
+        minus_norm(1, [2, 3])
         add_regroup(0)
-        prod_gpsimd(1)
-        stage_std_rows(1, (0, 1))
-        hook("start")
+        product_tile(1)
+        product_gpsimd(1, 2, J, 0)
+        bn(1, 2, 0)
+        bn(1, 2, 1)
+        bn(1, 3, 0)
+        aggregate(1, 2)
+        bn(1, 3, 1)
+        product0_vector(1, 0)
+        aggregate(1, 3)
+        product0_vector(1, 1)
+        scalar_image1()
+
         for u in range(UNITS - 2):
             nxt = u + 1
-            prod_vector(nxt)
-            for b in range(B):
-                if late_aggr.get(b):
-                    aggregate(b, 0)
-                    late_aggr[b] = False
-            hook((u, "a"))
+            if nxt > 1:
+                product_vector(nxt)
+            if u == 1:
+                aggregate(2, 3)
+            if u == 2:
+                scalar_image2()
             quantise(u)
             if u == 0:
                 weights_quantise()
-                nc.vector.tensor_copy(out=b_f[:], in_=b_bf[:])
             multiply(u)
             stage_std(u + 2)
-            hook((u, "b"))
+            if u == 4:
+                scalar_image3()
             add_regroup(nxt)
-            prod_gpsimd(nxt + 1)
+            product_gpsimd_unit(nxt + 1)
             finish(u)
-            hook((u, "c"))
+            if u == 0:
+                bn(2, 3, 0)
+                bn(2, 3, 1)
 
-        prod_vector(7)
+        product_vector(7)
         quantise(6)
         multiply(6)
         add_regroup(7)
-        exit_bank(6, 0, True)
-        exit_bank(6, 1, True)
+        exit_part(6, 0, 0, HALF, True)
+        exit_part(6, 1, 0, HALF, True)
         quantise(7)
         multiply(7)
-        exit_bank(6, 2, True)
-        exit_bank(6, 3, True)
+        exit_part(6, 2, 0, HALF, True)
+        exit_part(6, 3, 0, HALF, True)
         for j in range(J - 1):
-            exit_bank(7, j, True)
-        exit_part(7, J - 1, 0, HALF // 2)
-        exit_part(7, J - 1, HALF // 2, HALF)
+            exit_part(7, j, 0, HALF, True)
+        exit_part(7, J - 1, 0, HALF // 2, True)
+        exit_part(7, J - 1, HALF // 2, HALF, True)

@@ -22,7 +22,8 @@ EPS = 1e-5
 FLOPS = 2 * C * C * B * NPIX
 
 NS = [1, 2, 3, 4]
-VC = [0, 0, 128, 224, 224, 224, 224, 224]
+VC = [0, 0, 168, 216, 216, 216, 224, 208]
+SHARED = ((2, 3),)
 RUN = 8
 STAGED0 = (0, 2, 3)
 
@@ -76,8 +77,9 @@ def tile_aattn_pb_t_kernel(tc, content, mean, std, out_w, out_b, out):
         def mean_of(u):
             return m0_h[u][:] if u < 2 else m_t[u // 2][:, :, cols(u)]
 
-        for j, h in ((1, 0), (1, 1), (0, 0), (2, 0), (0, 1), (2, 1), (3, 0), (3, 1)):
+        for j, h in ((1, 0), (1, 1), (0, 0), (2, 0), (0, 1), (2, 1)):
             nc.sync.dma_start(out=x_t[0][:, j, h * HALF:(h + 1) * HALF], in_=xv[0][:, j, h * HALF:(h + 1) * HALF])
+        nc.sync.dma_start(out=x_t[0][:, 3, :], in_=xv[0][:, 3, :])
         nc.sync.dma_start(out=s0_h[0][:], in_=sv[0][:, :, 0:HALF])
         nc.sync.dma_start(out=x_t[1][:, 0:2, :], in_=xv[1][:, 0:2, :])
         nc.sync.dma_start(out=m0_h[0][:], in_=mv[0][:, :, 0:HALF])
@@ -102,6 +104,9 @@ def tile_aattn_pb_t_kernel(tc, content, mean, std, out_w, out_b, out):
         ssq = [keep.tile([P, J], F32, name="ssq%d" % b) for b in range(B)]
         st_t = [keep.tile([P, J, 2, 6], F32, name="st%d" % b) for b in range(B)]
         ag_t = [keep.tile([P, J, 2], F32, name="ag%d" % b) for b in range(B)]
+
+        for b, j in SHARED:
+            nc.vector.memset(st_t[b][:, j, 1, 0:1], float(HALF))
 
         def sum_scalar(b, j):
             junk = junkp.tile([P, NPIX], BF16, name="junk")
@@ -136,7 +141,18 @@ def tile_aattn_pb_t_kernel(tc, content, mean, std, out_w, out_b, out):
             nc.vector.bn_stats(out=st_t[b][:, j, h, :], in_=x_t[b][:, j, h * HALF:(h + 1) * HALF])
 
         def aggregate(b, j):
-            nc.vector.bn_aggr(out=ag_t[b][:, j, :], in_=st_t[b][:, j, :, :].rearrange("p c s -> p (c s)"))
+            n = 9 if (b, j) in SHARED else 12
+            nc.vector.bn_aggr(out=ag_t[b][:, j, :], in_=st_t[b][:, j, :, :].rearrange("p c s -> p (c s)")[:, 0:n])
+
+        def half_sum_scalar(b, j):
+            junk = junkp.tile([P, NPIX], BF16, name="junk")
+            nc.scalar.activation(out=junk[:, 0:HALF], in_=x_t[b][:, j, HALF:NPIX], func=ACT.Identity, scale=1.0 / HALF,
+                                 accum_out=st_t[b][:, j, 1, 1:2])
+
+        def half_square_scalar(b, j):
+            junk = junkp.tile([P, NPIX], BF16, name="junk")
+            nc.scalar.activation(out=junk[:, 0:HALF], in_=x_t[b][:, j, HALF:NPIX], func=ACT.Square, scale=-1.0,
+                                 bias=st_t[b][:, j, 1, 1:2], accum_out=st_t[b][:, j, 1, 2:3])
 
         nm_u = {}
         pr_u = {}
@@ -259,9 +275,15 @@ def tile_aattn_pb_t_kernel(tc, content, mean, std, out_w, out_b, out):
             if store:
                 nc.sync.dma_start(out=ov[b][:, j:j + 1, c0 + lo:c0 + hi], in_=ot[:, j:j + 1, lo:hi])
 
-        def finish(u):
-            for j in range(J):
-                exit_part(u, j, 0, HALF, False)
+        left = {u: 0 for u in range(UNITS)}
+
+        def exit_bank(u, j):
+            exit_part(u, j, 0, HALF, False)
+            left[u] = j + 1
+
+        def exit_rest(u):
+            for j in range(left[u], J):
+                exit_bank(u, j)
             nc.sync.dma_start(out=ov[u // 2][:, :, cols(u)], in_=ot_u[u][:])
 
         w_g = keep.tile([P, C * J], BF16, name="w_g", align_bytes=64)
@@ -311,28 +333,39 @@ def tile_aattn_pb_t_kernel(tc, content, mean, std, out_w, out_b, out):
             for j in range(J):
                 norm_row(3, j, 0, HALF)
 
-        def scalar_image2():
+        def scalar_image2(first):
+            if not first:
+                scalar_image2_rest()
+                return
             for j in range(3):
                 sum_scalar(2, j)
-            rstd_vector(2, 3, J)
+            half_sum_scalar(2, 3)
             square_scalar(2, 0)
-            negate_rstd(2, 3, J)
+            half_square_scalar(2, 3)
+
+        def scalar_image2_rest():
             square_scalar(2, 1)
-            nbias_row(2, 3)
+            rstd_scalar(2, 0, 1)
             square_scalar(2, 2)
-            rstd_scalar(2, 0, 2)
-            norm_tile(4)
-            norm_row(4, 3, 0, HALF)
             nbias_row(2, 0)
+            rstd_scalar(2, 1, 2)
+            norm_tile(4)
+            norm_row(4, 0, VC[4], HALF)
             nbias_row(2, 1)
             rstd_scalar(2, 2, 3)
-            norm_tile(5)
-            norm_row(5, 3, 0, HALF)
-            norm_row(4, 0, 0, HALF)
+            rstd_vector(2, 3, J)
+            norm_row(4, 0, 0, VC[4])
+            norm_row(4, 1, VC[4], HALF)
             nbias_row(2, 2)
-            norm_row(4, 1, 0, HALF)
-            norm_row(4, 2, 0, HALF)
-            for j in range(3):
+            negate_rstd(2, 3, J)
+            norm_row(4, 1, 0, VC[4])
+            norm_row(4, 2, VC[4], HALF)
+            nbias_row(2, 3)
+            norm_row(4, 2, 0, VC[4])
+            norm_row(4, 3, VC[4], HALF)
+            norm_row(4, 3, 0, VC[4])
+            norm_tile(5)
+            for j in range(J):
                 norm_row(5, j, 0, HALF)
 
         def scalar_image3():
@@ -410,32 +443,33 @@ def tile_aattn_pb_t_kernel(tc, content, mean, std, out_w, out_b, out):
         product0_vector(1, 1)
         scalar_image1()
 
-        for u in range(UNITS - 2):
-            nxt = u + 1
-            if nxt > 1:
-                product_vector(nxt)
-            if u == 1:
-                aggregate(2, 3)
-            if u == 2:
-                scalar_image2()
-            quantise(u)
-            if u == 0:
-                weights_quantise()
-            multiply(u)
-            stage_std(u + 2)
-            if u == 4:
+        quantise(0)
+        weights_quantise()
+        multiply(0)
+        stage_std(2)
+        add_regroup(1)
+        for n in range(2, UNITS):
+            m = n - 1
+            o = n - 2
+            if n == 4:
+                scalar_image2(False)
+            if n == 6:
                 scalar_image3()
-            add_regroup(nxt)
-            product_gpsimd_unit(nxt + 1)
-            finish(u)
-            if u == 0:
+            product_gpsimd_unit(n)
+            exit_rest(o)
+            if n == 2:
                 bn(2, 3, 0)
-                bn(2, 3, 1)
+            if n == 3:
+                scalar_image2(True)
+            product_vector(n)
+            if n == 3:
+                aggregate(2, 3)
+            quantise(m)
+            multiply(m)
+            if n + 1 < UNITS:
+                stage_std(n + 1)
+            add_regroup(n)
 
-        product_vector(7)
-        quantise(6)
-        multiply(6)
-        add_regroup(7)
         exit_part(6, 0, 0, HALF, True)
         exit_part(6, 1, 0, HALF, True)
         quantise(7)

@@ -22,7 +22,7 @@ EPS = 1e-5
 FLOPS = 2 * C * C * B * NPIX
 
 NS = [1, 2, 3, 4]
-VC = [0, 0, 168, 216, 216, 216, 224, 208]
+VC = [0, 0, 168, 208, 208, 208, 208, 208]
 SHARED = ((2, 3),)
 RUN = 8
 STAGED0 = (0, 2, 3)
@@ -41,8 +41,7 @@ def tile_aattn_pb_t_kernel(tc, content, mean, std, out_w, out_b, out):
         keep = ctx.enter_context(tc.tile_pool(name="keep", bufs=1))
         junkp = ctx.enter_context(tc.tile_pool(name="junkp", bufs=4))
         nmp = ctx.enter_context(tc.tile_pool(name="nmp", bufs=4))
-        mp = ctx.enter_context(tc.tile_pool(name="mp", bufs=1))
-        ogp = ctx.enter_context(tc.tile_pool(name="ogp", bufs=2))
+        ring = ctx.enter_context(tc.tile_pool(name="ring", bufs=3))
         cdp = ctx.enter_context(tc.tile_pool(name="cdp", bufs=2))
         otp = ctx.enter_context(tc.tile_pool(name="otp", bufs=4))
         psum = ctx.enter_context(tc.psum_pool(name="psum", bufs=8))
@@ -216,7 +215,7 @@ def tile_aattn_pb_t_kernel(tc, content, mean, std, out_w, out_b, out):
                 st_u[u][j] = st
 
         def product_tile(u):
-            pr_u[u] = mp.tile([P, J, HALF], F32, name="pr")
+            pr_u[u] = ring.tile([P, J, HALF], F32, name="pr", tag="ring", align_bytes=64)
 
         def product_gpsimd(u, lo, hi, c0):
             nc.gpsimd.tensor_tensor(out=pr_u[u][:, lo:hi, c0:HALF], in0=nm_u[u][:, lo:hi, c0:HALF],
@@ -224,7 +223,7 @@ def tile_aattn_pb_t_kernel(tc, content, mean, std, out_w, out_b, out):
 
         def product_gpsimd_unit(u):
             product_tile(u)
-            for lo, hi in (((0, 2), (2, J)) if u == 6 else ((0, J),)):
+            for lo, hi in (((0, 3), (3, J)) if u in (4, 6) else ((0, J),)):
                 product_gpsimd(u, lo, hi, VC[u])
 
         def product0_vector(u, j):
@@ -238,7 +237,7 @@ def tile_aattn_pb_t_kernel(tc, content, mean, std, out_w, out_b, out):
                                         in0=nm_u[u][:, 2 * h:2 * h + 2, 0:VC[u]], in1=st_u[u][h][:], op=ALU.mult)
 
         def add_regroup(u):
-            og = ogp.tile([P, HALF * J], BF16, name="og", align_bytes=64)
+            og = ring.tile([P, HALF * J], BF16, name="og", tag="ring", align_bytes=64)
             og_u[u] = og
             nc.vector.tensor_tensor(
                 out=og[:].rearrange("p (c i t) -> p c t i", i=RUN, t=J),
@@ -286,7 +285,7 @@ def tile_aattn_pb_t_kernel(tc, content, mean, std, out_w, out_b, out):
                 exit_bank(u, j)
             nc.sync.dma_start(out=ov[u // 2][:, :, cols(u)], in_=ot_u[u][:])
 
-        w_g = keep.tile([P, C * J], BF16, name="w_g", align_bytes=64)
+        w_g = {}
         w_cd = keep.tile([P, C], U32, name="w_cd", align_bytes=64)
         w_sc = keep.tile([P, C], U8, name="w_sc", align_bytes=64)
         wt_h = []
@@ -301,12 +300,14 @@ def tile_aattn_pb_t_kernel(tc, content, mean, std, out_w, out_b, out):
                 wt_h.append(wt)
 
         def weights_copy(hh):
-            g32 = w_g[:].bitcast(F32)
+            if hh == 0:
+                w_g[0] = ring.tile([P, C * J], BF16, name="w_g", tag="ring", align_bytes=64)
+            g32 = w_g[0][:].bitcast(F32)
             nc.scalar.copy(out=g32[:, hh * 512:(hh + 1) * 512].rearrange("p (a m u) -> p a m u", a=2, u=2),
                            in_=wt_h[hh][:].rearrange("p a u m -> p a m u"))
 
         def weights_quantise():
-            nc.vector.quantize_mx(out=w_cd[:].bitcast(FP8X4), scales=w_sc[:], in_=w_g[:])
+            nc.vector.quantize_mx(out=w_cd[:].bitcast(FP8X4), scales=w_sc[:], in_=w_g[0][:])
 
         def scalar_image1():
             sum_scalar(1, 1)
@@ -341,35 +342,34 @@ def tile_aattn_pb_t_kernel(tc, content, mean, std, out_w, out_b, out):
                 sum_scalar(2, j)
             half_sum_scalar(2, 3)
             square_scalar(2, 0)
+            square_scalar(2, 1)
+            rstd_scalar(2, 0, 1)
             half_square_scalar(2, 3)
 
         def scalar_image2_rest():
-            square_scalar(2, 1)
-            rstd_scalar(2, 0, 1)
-            square_scalar(2, 2)
             nbias_row(2, 0)
+            square_scalar(2, 2)
             rstd_scalar(2, 1, 2)
             norm_tile(4)
             norm_row(4, 0, VC[4], HALF)
             nbias_row(2, 1)
             rstd_scalar(2, 2, 3)
             rstd_vector(2, 3, J)
-            norm_row(4, 0, 0, VC[4])
             norm_row(4, 1, VC[4], HALF)
             nbias_row(2, 2)
             negate_rstd(2, 3, J)
-            norm_row(4, 1, 0, VC[4])
             norm_row(4, 2, VC[4], HALF)
             nbias_row(2, 3)
-            norm_row(4, 2, 0, VC[4])
+            norm_row(4, 0, 0, VC[4])
             norm_row(4, 3, VC[4], HALF)
-            norm_row(4, 3, 0, VC[4])
+            for j in (1, 2, 3):
+                norm_row(4, j, 0, VC[4])
             norm_tile(5)
             for j in range(J):
                 norm_row(5, j, 0, HALF)
 
         def scalar_image3():
-            for j in range(J):
+            for j in range(3):
                 sum_scalar(3, j)
             square_scalar(3, 0)
             square_scalar(3, 1)
@@ -377,19 +377,22 @@ def tile_aattn_pb_t_kernel(tc, content, mean, std, out_w, out_b, out):
             square_scalar(3, 2)
             nbias_row(3, 0)
             rstd_scalar(3, 1, 2)
-            square_scalar(3, 3)
+            sum_scalar(3, 3)
             nbias_row(3, 1)
+            rstd_scalar(3, 2, 3)
             norm_tile(6)
             norm_row(6, 0, VC[6], HALF)
-            rstd_scalar(3, 2, J)
-            norm_row(6, 1, VC[6], HALF)
             nbias_row(3, 2)
-            nbias_row(3, 3)
-            norm_row(6, 0, 0, VC[6])
+            norm_row(6, 1, VC[6], HALF)
             norm_row(6, 2, VC[6], HALF)
+            square_scalar(3, 3)
+            norm_row(6, 0, 0, VC[6])
+            rstd_scalar(3, 3, J)
+            norm_row(6, 1, 0, VC[6])
+            nbias_row(3, 3)
+            norm_row(6, 2, 0, VC[6])
             norm_row(6, 3, VC[6], HALF)
-            for j in (1, 2, 3):
-                norm_row(6, j, 0, VC[6])
+            norm_row(6, 3, 0, VC[6])
             norm_tile(7)
             for j in range(J):
                 norm_row(7, j, 0, HALF)
@@ -456,14 +459,14 @@ def tile_aattn_pb_t_kernel(tc, content, mean, std, out_w, out_b, out):
             if n == 6:
                 scalar_image3()
             product_gpsimd_unit(n)
+            if n == 3:
+                scalar_image2(True)
             exit_rest(o)
             if n == 2:
                 bn(2, 3, 0)
             if n == 3:
-                scalar_image2(True)
-            product_vector(n)
-            if n == 3:
                 aggregate(2, 3)
+            product_vector(n)
             quantise(m)
             multiply(m)
             if n + 1 < UNITS:

@@ -22,7 +22,7 @@ EPS = 1e-5
 FLOPS = 2 * C * C * B * NPIX
 
 NS = [1, 2, 3, 4]
-VC = [0, 0, 168, 208, 208, 208, 208, 208]
+VC = [0, 0, 168, 184, 192, 184, 192, 184]
 SHARED = ((2, 3),)
 RUN = 8
 STAGED0 = (0, 2, 3)
@@ -83,12 +83,14 @@ def tile_aattn_pb_t_kernel(tc, content, mean, std, out_w, out_b, out):
         nc.sync.dma_start(out=x_t[1][:, 0:2, :], in_=xv[1][:, 0:2, :])
         nc.sync.dma_start(out=m0_h[0][:], in_=mv[0][:, :, 0:HALF])
         nc.sync.dma_start(out=x_t[1][:, 2:4, :], in_=xv[1][:, 2:4, :])
-        nc.sync.dma_start(out=s0_h[1][:], in_=sv[0][:, :, HALF:NPIX])
+        nc.sync.dma_start(out=s0_h[1][:, 2:4, :], in_=sv[0][:, 2:4, HALF:NPIX])
         nc.sync.dma_start(out=w_sb[:], in_=wv)
+        nc.sync.dma_start(out=s0_h[1][:, 0:2, :], in_=sv[0][:, 0:2, HALF:NPIX])
         nc.sync.dma_start(out=m0_h[1][:], in_=mv[0][:, :, HALF:NPIX])
         nc.sync.dma_start(out=b_bf[:], in_=bv)
         nc.sync.dma_start(out=s_t[1][:], in_=sv[1])
-        nc.sync.dma_start(out=x_t[2][:], in_=xv[2])
+        nc.sync.dma_start(out=x_t[2][:, 0:2, :], in_=xv[2][:, 0:2, :])
+        nc.sync.dma_start(out=x_t[2][:, 2:4, :], in_=xv[2][:, 2:4, :])
         nc.sync.dma_start(out=m_t[1][:], in_=mv[1])
         nc.sync.dma_start(out=s_t[2][:], in_=sv[2])
         nc.sync.dma_start(out=x_t[3][:], in_=xv[3])
@@ -226,9 +228,9 @@ def tile_aattn_pb_t_kernel(tc, content, mean, std, out_w, out_b, out):
             for lo, hi in (((0, 3), (3, J)) if u in (4, 6) else ((0, J),)):
                 product_gpsimd(u, lo, hi, VC[u])
 
-        def product0_vector(u, j):
-            nc.vector.scalar_tensor_tensor(out=pr_u[u][:, j, :], in0=nm_u[u][:, j, :], scalar=rstd[0][:, j:j + 1],
-                                           in1=st_u[u][j][:] if j in st_u.get(u, {}) else std_of(u)[:, j, :],
+        def product0_vector(u, j, lo=0, hi=HALF):
+            nc.vector.scalar_tensor_tensor(out=pr_u[u][:, j, lo:hi], in0=nm_u[u][:, j, lo:hi], scalar=rstd[0][:, j:j + 1],
+                                           in1=(st_u[u][j][:, lo:hi] if j in st_u.get(u, {}) else std_of(u)[:, j, lo:hi]),
                                            op0=ALU.mult, op1=ALU.mult)
 
         def product_vector(u):
@@ -236,13 +238,13 @@ def tile_aattn_pb_t_kernel(tc, content, mean, std, out_w, out_b, out):
                 nc.vector.tensor_tensor(out=pr_u[u][:, 2 * h:2 * h + 2, 0:VC[u]],
                                         in0=nm_u[u][:, 2 * h:2 * h + 2, 0:VC[u]], in1=st_u[u][h][:], op=ALU.mult)
 
-        def add_regroup(u):
-            og = ring.tile([P, HALF * J], BF16, name="og", tag="ring", align_bytes=64)
-            og_u[u] = og
+        def add_regroup(u, lo=0, hi=HALF):
+            if u not in og_u:
+                og_u[u] = ring.tile([P, HALF * J], BF16, name="og", tag="ring", align_bytes=64)
             nc.vector.tensor_tensor(
-                out=og[:].rearrange("p (c i t) -> p c t i", i=RUN, t=J),
-                in0=mean_of(u).rearrange("p t (c i) -> p c t i", i=RUN),
-                in1=pr_u[u][:].rearrange("p t (c i) -> p c t i", i=RUN),
+                out=og_u[u][:, lo * J:hi * J].rearrange("p (c i t) -> p c t i", i=RUN, t=J),
+                in0=mean_of(u)[:, :, lo:hi].rearrange("p t (c i) -> p c t i", i=RUN),
+                in1=pr_u[u][:, :, lo:hi].rearrange("p t (c i) -> p c t i", i=RUN),
                 op=(ALU.subtract if u < 2 else ALU.add))
 
         def quantise(u):
@@ -317,18 +319,21 @@ def tile_aattn_pb_t_kernel(tc, content, mean, std, out_w, out_b, out):
             weights_transpose()
             weights_copy(0)
             rstd_scalar(1, 1, 2)
-            rstd_vector(1, 2, J)
+            rstd_vector(1, 2, 3)
             nbias_row(1, 0)
             weights_copy(1)
+            rstd_vector(1, 3, J)
             nbias_row(1, 1)
-            negate_rstd(1, 2, J)
             norm_tile(2)
             norm_row(2, 0, VC[2], HALF)
+            negate_rstd(1, 2, J)
+            norm_row(2, 1, VC[2], HALF)
             nbias_row(1, 2)
             nbias_row(1, 3)
-            for j in (1, 2, 3):
+            norm_row(2, 0, 0, VC[2])
+            for j in (2, 3):
                 norm_row(2, j, VC[2], HALF)
-            for j in range(J):
+            for j in (1, 2, 3):
                 norm_row(2, j, 0, VC[2])
             norm_tile(3)
             for j in range(J):
@@ -345,24 +350,25 @@ def tile_aattn_pb_t_kernel(tc, content, mean, std, out_w, out_b, out):
             square_scalar(2, 1)
             rstd_scalar(2, 0, 1)
             half_square_scalar(2, 3)
-
-        def scalar_image2_rest():
+            rstd_scalar(2, 1, 2)
             nbias_row(2, 0)
             square_scalar(2, 2)
-            rstd_scalar(2, 1, 2)
+            nbias_row(2, 1)
+
+        def scalar_image2_rest():
             norm_tile(4)
             norm_row(4, 0, VC[4], HALF)
-            nbias_row(2, 1)
             rstd_scalar(2, 2, 3)
             rstd_vector(2, 3, J)
             norm_row(4, 1, VC[4], HALF)
             nbias_row(2, 2)
             negate_rstd(2, 3, J)
+            norm_row(4, 0, 0, VC[4])
             norm_row(4, 2, VC[4], HALF)
             nbias_row(2, 3)
-            norm_row(4, 0, 0, VC[4])
+            norm_row(4, 1, 0, VC[4])
             norm_row(4, 3, VC[4], HALF)
-            for j in (1, 2, 3):
+            for j in (2, 3):
                 norm_row(4, j, 0, VC[4])
             norm_tile(5)
             for j in range(J):
@@ -431,9 +437,11 @@ def tile_aattn_pb_t_kernel(tc, content, mean, std, out_w, out_b, out):
         centre_gpsimd(1, 0)
         product0_vector(0, 0)
         product0_vector(0, 2)
-        product0_vector(0, 3)
+        product0_vector(0, 3, 0, HALF // 2)
+        product0_vector(0, 3, HALF // 2, HALF)
         minus_norm(1, [2, 3])
-        add_regroup(0)
+        add_regroup(0, 0, HALF // 2)
+        add_regroup(0, HALF // 2, HALF)
         product_tile(1)
         product_gpsimd(1, 2, J, 0)
         bn(1, 2, 0)
@@ -464,9 +472,9 @@ def tile_aattn_pb_t_kernel(tc, content, mean, std, out_w, out_b, out):
             exit_rest(o)
             if n == 2:
                 bn(2, 3, 0)
+            product_vector(n)
             if n == 3:
                 aggregate(2, 3)
-            product_vector(n)
             quantise(m)
             multiply(m)
             if n + 1 < UNITS:

from contextlib import ExitStack

import concourse.mybir as mybir
from concourse.masks import make_identity

F32 = mybir.dt.float32
BF16 = mybir.dt.bfloat16
U32 = mybir.dt.uint32
U8 = mybir.dt.uint8
FP8X4 = mybir.dt.float8_e4m3fn_x4
ALU = mybir.AluOpType
ACT = mybir.ActivationFunctionType

B = 4
C = 512
NPIX = 1024
P = 128
J = 4
HALF = 512
UNITS = 2 * B
EPS = 1e-5
FLOPS = 2 * C * C * B * NPIX

NS = [1, 2, 3, 4]
VC = [0, 0, 168, 184, 192, 184, 192, 184]
SHARED = ((2, 3),)
RUN = 8
STAGED0 = (0, 2, 3)


def tile_aattn_pb_t_kernel(tc, content, mean, std, out_w, out_b, out):
    nc = tc.nc
    xv = content.rearrange("b (p j) h w -> b p j (h w)", j=J)
    mv = mean.rearrange("b (p j) h w -> b p j (h w)", j=J)
    sv = std.rearrange("b (p j) h w -> b p j (h w)", j=J)
    ov = out.rearrange("b (p j) h w -> b p j (h w)", j=J)
    wv = out_w.rearrange("(m j) c -> m j c", j=J)
    bv = out_b.rearrange("(p j) -> p j", j=J)

    with ExitStack() as ctx:
        keep = ctx.enter_context(tc.tile_pool(name="keep", bufs=1))
        junkp = ctx.enter_context(tc.tile_pool(name="junkp", bufs=4))
        nmp = ctx.enter_context(tc.tile_pool(name="nmp", bufs=4))
        ring = ctx.enter_context(tc.tile_pool(name="ring", bufs=3))
        cdp = ctx.enter_context(tc.tile_pool(name="cdp", bufs=2))
        otp = ctx.enter_context(tc.tile_pool(name="otp", bufs=4))
        psum = ctx.enter_context(tc.psum_pool(name="psum", bufs=8))
        ctx.enter_context(tc.manual_schedule())

        eps_t = keep.tile([P, 1], F32, name="eps_t")
        one_t = keep.tile([P, 1], F32, name="one_t")
        warm_t = keep.tile([P, 1], F32, name="warm_t")
        minus_t = keep.tile([P, 1], F32, name="minus_t")
        nc.vector.memset(one_t[:], 1.0)
        nc.vector.memset(eps_t[:], EPS)
        nc.scalar.activation(out=warm_t[:], in_=one_t[:], func=ACT.Abs_reciprocal_sqrt)
        ident_bf = keep.tile([P, P], BF16, name="ident_bf")
        make_identity(nc, ident_bf[:])
        ident = keep.tile([P, P], F32, name="ident")
        make_identity(nc, ident[:])

        x_t = [keep.tile([P, J, NPIX], BF16, name="x%d" % b) for b in range(B)]
        s_t = [None] + [keep.tile([P, J, NPIX], BF16, name="s%d" % b) for b in range(1, B)]
        m_t = [None] + [keep.tile([P, J, NPIX], BF16, name="m%d" % b) for b in range(1, B)]
        s0_h = [keep.tile([P, J, HALF], BF16, name="s0h%d" % h) for h in range(2)]
        m0_h = [keep.tile([P, J, HALF], BF16, name="m0h%d" % h) for h in range(2)]
        w_sb = keep.tile([P, J, C], BF16, name="w_sb")
        b_bf = keep.tile([P, J], BF16, name="b_bf")

        def cols(u):
            return slice((u % 2) * HALF, (u % 2 + 1) * HALF)

        def std_of(u):
            return s0_h[u][:] if u < 2 else s_t[u // 2][:, :, cols(u)]

        def mean_of(u):
            return m0_h[u][:] if u < 2 else m_t[u // 2][:, :, cols(u)]

        for j, h in ((1, 0), (1, 1), (0, 0), (2, 0), (0, 1), (2, 1)):
            nc.sync.dma_start(out=x_t[0][:, j, h * HALF:(h + 1) * HALF], in_=xv[0][:, j, h * HALF:(h + 1) * HALF])
        nc.sync.dma_start(out=x_t[0][:, 3, :], in_=xv[0][:, 3, :])
        nc.sync.dma_start(out=s0_h[0][:], in_=sv[0][:, :, 0:HALF])
        nc.sync.dma_start(out=x_t[1][:, 0:2, :], in_=xv[1][:, 0:2, :])
        nc.sync.dma_start(out=m0_h[0][:], in_=mv[0][:, :, 0:HALF])
        nc.sync.dma_start(out=x_t[1][:, 2:4, :], in_=xv[1][:, 2:4, :])
        nc.sync.dma_start(out=s0_h[1][:, 2:4, :], in_=sv[0][:, 2:4, HALF:NPIX])
        nc.sync.dma_start(out=w_sb[:], in_=wv)
        nc.sync.dma_start(out=s0_h[1][:, 0:2, :], in_=sv[0][:, 0:2, HALF:NPIX])
        nc.sync.dma_start(out=m0_h[1][:], in_=mv[0][:, :, HALF:NPIX])
        nc.sync.dma_start(out=b_bf[:], in_=bv)
        nc.sync.dma_start(out=s_t[1][:], in_=sv[1])
        nc.sync.dma_start(out=x_t[2][:, 0:2, :], in_=xv[2][:, 0:2, :])
        nc.sync.dma_start(out=x_t[2][:, 2:4, :], in_=xv[2][:, 2:4, :])
        nc.sync.dma_start(out=m_t[1][:], in_=mv[1])
        nc.sync.dma_start(out=s_t[2][:], in_=sv[2])
        nc.sync.dma_start(out=x_t[3][:], in_=xv[3])
        nc.sync.dma_start(out=m_t[2][:], in_=mv[2])
        nc.sync.dma_start(out=s_t[3][:], in_=sv[3])
        nc.sync.dma_start(out=m_t[3][:], in_=mv[3])

        rstd = [keep.tile([P, J], F32, name="rstd%d" % b) for b in range(B)]
        nbias = [keep.tile([P, J], F32, name="nbias%d" % b) for b in range(B)]
        nrstd = [keep.tile([P, J], F32, name="nrstd%d" % b) for b in range(B)]
        nmean = [keep.tile([P, J], F32, name="nmean%d" % b) for b in range(B)]
        ssq = [keep.tile([P, J], F32, name="ssq%d" % b) for b in range(B)]
        st_t = [keep.tile([P, J, 2, 6], F32, name="st%d" % b) for b in range(B)]
        ag_t = [keep.tile([P, J, 2], F32, name="ag%d" % b) for b in range(B)]

        for b, j in SHARED:
            nc.vector.memset(st_t[b][:, j, 1, 0:1], float(HALF))

        def sum_scalar(b, j):
            junk = junkp.tile([P, NPIX], BF16, name="junk")
            nc.scalar.activation(out=junk[:], in_=x_t[b][:, j, :], func=ACT.Identity, scale=-1.0 / NPIX,
                                 accum_out=nmean[b][:, j:j + 1])

        def square_scalar(b, j):
            junk = junkp.tile([P, NPIX], BF16, name="junk")
            nc.scalar.activation(out=junk[:], in_=x_t[b][:, j, :], func=ACT.Square, bias=nmean[b][:, j:j + 1],
                                 accum_out=ssq[b][:, j:j + 1])

        def rstd_scalar(b, lo, hi):
            nc.scalar.activation(out=rstd[b][:, lo:hi], in_=ssq[b][:, lo:hi], func=ACT.Abs_reciprocal_sqrt,
                                 scale=1.0 / (NPIX - 1), bias=eps_t[:, 0:1])

        def rstd_vector(b, lo, hi):
            nc.scalar.activation(out=rstd[b][:, lo:hi], in_=ag_t[b][:, lo:hi, 1], func=ACT.Abs_reciprocal_sqrt,
                                 scale=float(NPIX) / (NPIX - 1), bias=eps_t[:, 0:1])

        def negate_rstd(b, lo, hi):
            nc.scalar.mul(out=nrstd[b][:, lo:hi], in_=rstd[b][:, lo:hi], mul=-1.0)

        def nbias_row(b, j):
            if j < NS[b]:
                nc.scalar.activation(out=nbias[b][:, j:j + 1], in_=nmean[b][:, j:j + 1], func=ACT.Identity,
                                     scale=rstd[b][:, j:j + 1])
            else:
                nc.scalar.activation(out=nbias[b][:, j:j + 1], in_=ag_t[b][:, j, 0:1], func=ACT.Identity,
                                     scale=nrstd[b][:, j:j + 1])

        def bn(b, j, h):
            nc.vector.bn_stats(out=st_t[b][:, j, h, :], in_=x_t[b][:, j, h * HALF:(h + 1) * HALF])

        def aggregate(b, j):
            n = 9 if (b, j) in SHARED else 12
            nc.vector.bn_aggr(out=ag_t[b][:, j, :], in_=st_t[b][:, j, :, :].rearrange("p c s -> p (c s)")[:, 0:n])

        def half_sum_scalar(b, j):
            junk = junkp.tile([P, NPIX], BF16, name="junk")
            nc.scalar.activation(out=junk[:, 0:HALF], in_=x_t[b][:, j, HALF:NPIX], func=ACT.Identity, scale=1.0 / HALF,
                                 accum_out=st_t[b][:, j, 1, 1:2])

        def half_square_scalar(b, j):
            junk = junkp.tile([P, NPIX], BF16, name="junk")
            nc.scalar.activation(out=junk[:, 0:HALF], in_=x_t[b][:, j, HALF:NPIX], func=ACT.Square, scale=-1.0,
                                 bias=st_t[b][:, j, 1, 1:2], accum_out=st_t[b][:, j, 1, 2:3])

        nm_u = {}
        pr_u = {}
        og_u = {}
        cd_u = {}
        ac_u = {}
        st_u = {}
        ot_u = {}

        nm0 = keep.tile([P, J, NPIX], F32, name="nm0")
        nm_u[0] = nm0[:, :, 0:HALF]
        nm_u[1] = nm0[:, :, HALF:NPIX]
        mu0 = keep.tile([P, 1], F32, name="mu0")

        def mean0(j):
            return mu0[:, 0:1] if j == 0 else ag_t[0][:, j, 0:1]

        def centre_scalar(u, j):
            nc.scalar.activation(out=nm_u[u][:, j, :], in_=x_t[0][:, j, cols(u)], func=ACT.Identity,
                                 scale=-1.0, bias=mean0(j))

        def centre_gpsimd(u, j):
            nc.gpsimd.tensor_scalar(out=nm_u[u][:, j, :], in0=x_t[0][:, j, cols(u)],
                                    scalar1=(-1.0 if u == 0 else minus_t[:, 0:1]),
                                    scalar2=mean0(j), op0=ALU.mult, op1=ALU.add)

        def minus_norm(u, rows):
            lo, hi = rows[0], rows[-1] + 1
            negate_rstd(0, lo, hi)
            for j in rows:
                nc.scalar.activation(out=nbias[0][:, j:j + 1], in_=mean0(j), func=ACT.Identity,
                                     scale=rstd[0][:, j:j + 1])
            sum_scalar(1, 0)
            for j in rows:
                nc.scalar.activation(out=nm_u[u][:, j, :], in_=x_t[0][:, j, cols(u)], func=ACT.Identity,
                                     scale=nrstd[0][:, j:j + 1], bias=nbias[0][:, j:j + 1])

        def norm_row(u, j, lo, hi):
            b = u // 2
            c0 = (u % 2) * HALF
            nc.scalar.activation(out=nm_u[u][:, j, lo:hi], in_=x_t[b][:, j, c0 + lo:c0 + hi], func=ACT.Identity,
                                 scale=rstd[b][:, j:j + 1], bias=nbias[b][:, j:j + 1])

        def norm_tile(u):
            nm_u[u] = nmp.tile([P, J, HALF], F32, name="nm")

        def stage_std(u):
            st_u[u] = []
            for h in range(2):
                st = psum.tile([P, 2, VC[u]], F32, name="st", tag="bank")
                for r in range(2):
                    nc.tensor.matmul(out=st[:, r, :], lhsT=ident_bf[:], rhs=std_of(u)[:, 2 * h + r, 0:VC[u]],
                                     start=True, stop=True)
                st_u[u].append(st)

        def stage_std_rows(u, rows):
            st_u[u] = {}
            for j in rows:
                st = psum.tile([P, HALF], F32, name="st", tag="bank")
                nc.tensor.matmul(out=st[:], lhsT=ident_bf[:], rhs=std_of(u)[:, j, :], start=True, stop=True)
                st_u[u][j] = st

        def product_tile(u):
            pr_u[u] = ring.tile([P, J, HALF], F32, name="pr", tag="ring", align_bytes=64)

        def product_gpsimd(u, lo, hi, c0):
            nc.gpsimd.tensor_tensor(out=pr_u[u][:, lo:hi, c0:HALF], in0=nm_u[u][:, lo:hi, c0:HALF],
                                    in1=std_of(u)[:, lo:hi, c0:HALF], op=ALU.mult)

        def product_gpsimd_unit(u):
            product_tile(u)
            for lo, hi in (((0, 3), (3, J)) if u in (4, 6) else ((0, J),)):
                product_gpsimd(u, lo, hi, VC[u])

        def product0_vector(u, j, lo=0, hi=HALF):
            nc.vector.scalar_tensor_tensor(out=pr_u[u][:, j, lo:hi], in0=nm_u[u][:, j, lo:hi], scalar=rstd[0][:, j:j + 1],
                                           in1=(st_u[u][j][:, lo:hi] if j in st_u.get(u, {}) else std_of(u)[:, j, lo:hi]),
                                           op0=ALU.mult, op1=ALU.mult)

        def product_vector(u):
            for h in range(2):
                nc.vector.tensor_tensor(out=pr_u[u][:, 2 * h:2 * h + 2, 0:VC[u]],
                                        in0=nm_u[u][:, 2 * h:2 * h + 2, 0:VC[u]], in1=st_u[u][h][:], op=ALU.mult)

        def add_regroup(u, lo=0, hi=HALF):
            if u not in og_u:
                og_u[u] = ring.tile([P, HALF * J], BF16, name="og", tag="ring", align_bytes=64)
            nc.vector.tensor_tensor(
                out=og_u[u][:, lo * J:hi * J].rearrange("p (c i t) -> p c t i", i=RUN, t=J),
                in0=mean_of(u)[:, :, lo:hi].rearrange("p t (c i) -> p c t i", i=RUN),
                in1=pr_u[u][:, :, lo:hi].rearrange("p t (c i) -> p c t i", i=RUN),
                op=(ALU.subtract if u < 2 else ALU.add))

        def quantise(u):
            cd = cdp.tile([P, HALF], U32, name="cd", align_bytes=64)
            sc = cdp.tile([P, HALF], U8, name="sc", align_bytes=64)
            cd_u[u] = (cd, sc)
            nc.vector.quantize_mx(out=cd[:].bitcast(FP8X4), scales=sc[:], in_=og_u[u][:])

        def multiply(u):
            cd, sc = cd_u[u]
            accs = {}
            for j in range(J):
                acc = psum.tile([P, HALF], F32, name="acc", tag="bank")
                nc.tensor.matmul_mx(out=acc[:], lhsT=w_cd[:, j * P:(j + 1) * P].bitcast(FP8X4),
                                    lhsT_scale=w_sc[:, j * P:(j + 1) * P],
                                    rhs=cd[:].bitcast(FP8X4), rhs_scale=sc[:],
                                    start=True, stop=True)
                accs[j] = acc
            ac_u[u] = accs

        def exit_part(u, j, lo, hi, store):
            b = u // 2
            if u not in ot_u:
                ot_u[u] = otp.tile([P, J, HALF], F32, name="ot")
            ot = ot_u[u]
            c0 = (u % 2) * HALF
            nc.vector.scalar_tensor_tensor(out=ot[:, j, lo:hi], in0=x_t[b][:, j, c0 + lo:c0 + hi], scalar=b_bf[:, j:j + 1],
                                           in1=ac_u[u][j][:, lo:hi], op0=ALU.add, op1=ALU.add)
            if store:
                nc.sync.dma_start(out=ov[b][:, j:j + 1, c0 + lo:c0 + hi], in_=ot[:, j:j + 1, lo:hi])

        left = {u: 0 for u in range(UNITS)}

        def exit_bank(u, j):
            exit_part(u, j, 0, HALF, False)
            left[u] = j + 1

        def exit_rest(u):
            for j in range(left[u], J):
                exit_bank(u, j)
            nc.sync.dma_start(out=ov[u // 2][:, :, cols(u)], in_=ot_u[u][:])

        w_g = {}
        w_cd = keep.tile([P, C], U32, name="w_cd", align_bytes=64)
        w_sc = keep.tile([P, C], U8, name="w_sc", align_bytes=64)
        wt_h = []

        def weights_transpose():
            w32 = w_sb[:].bitcast(F32).rearrange("p j (q u) -> p j q u", u=2)
            for hh in range(2):
                wt = psum.tile([P, 2, 2, P], F32, name="wt", tag="bank")
                for a in range(2):
                    for u2 in range(2):
                        nc.tensor.transpose(wt[:, a, u2, :], w32[:, 2 * hh + a, :, u2], ident[:])
                wt_h.append(wt)

        def weights_copy(hh):
            if hh == 0:
                w_g[0] = ring.tile([P, C * J], BF16, name="w_g", tag="ring", align_bytes=64)
            g32 = w_g[0][:].bitcast(F32)
            nc.scalar.copy(out=g32[:, hh * 512:(hh + 1) * 512].rearrange("p (a m u) -> p a m u", a=2, u=2),
                           in_=wt_h[hh][:].rearrange("p a u m -> p a m u"))

        def weights_quantise():
            nc.vector.quantize_mx(out=w_cd[:].bitcast(FP8X4), scales=w_sc[:], in_=w_g[0][:])

        def scalar_image1():
            sum_scalar(1, 1)
            square_scalar(1, 0)
            square_scalar(1, 1)
            rstd_scalar(1, 0, 1)
            weights_transpose()
            weights_copy(0)
            rstd_scalar(1, 1, 2)
            rstd_vector(1, 2, 3)
            nbias_row(1, 0)
            weights_copy(1)
            rstd_vector(1, 3, J)
            nbias_row(1, 1)
            norm_tile(2)
            norm_row(2, 0, VC[2], HALF)
            negate_rstd(1, 2, J)
            norm_row(2, 1, VC[2], HALF)
            nbias_row(1, 2)
            nbias_row(1, 3)
            norm_row(2, 0, 0, VC[2])
            for j in (2, 3):
                norm_row(2, j, VC[2], HALF)
            for j in (1, 2, 3):
                norm_row(2, j, 0, VC[2])
            norm_tile(3)
            for j in range(J):
                norm_row(3, j, 0, HALF)

        def scalar_image2(first):
            if not first:
                scalar_image2_rest()
                return
            for j in range(3):
                sum_scalar(2, j)
            half_sum_scalar(2, 3)
            square_scalar(2, 0)
            square_scalar(2, 1)
            rstd_scalar(2, 0, 1)
            half_square_scalar(2, 3)
            rstd_scalar(2, 1, 2)
            nbias_row(2, 0)
            square_scalar(2, 2)
            nbias_row(2, 1)

        def scalar_image2_rest():
            norm_tile(4)
            norm_row(4, 0, VC[4], HALF)
            rstd_scalar(2, 2, 3)
            rstd_vector(2, 3, J)
            norm_row(4, 1, VC[4], HALF)
            nbias_row(2, 2)
            negate_rstd(2, 3, J)
            norm_row(4, 0, 0, VC[4])
            norm_row(4, 2, VC[4], HALF)
            nbias_row(2, 3)
            norm_row(4, 1, 0, VC[4])
            norm_row(4, 3, VC[4], HALF)
            for j in (2, 3):
                norm_row(4, j, 0, VC[4])
            norm_tile(5)
            for j in range(J):
                norm_row(5, j, 0, HALF)

        def scalar_image3():
            for j in range(3):
                sum_scalar(3, j)
            square_scalar(3, 0)
            square_scalar(3, 1)
            rstd_scalar(3, 0, 1)
            square_scalar(3, 2)
            nbias_row(3, 0)
            rstd_scalar(3, 1, 2)
            sum_scalar(3, 3)
            nbias_row(3, 1)
            rstd_scalar(3, 2, 3)
            norm_tile(6)
            norm_row(6, 0, VC[6], HALF)
            nbias_row(3, 2)
            norm_row(6, 1, VC[6], HALF)
            norm_row(6, 2, VC[6], HALF)
            square_scalar(3, 3)
            norm_row(6, 0, 0, VC[6])
            rstd_scalar(3, 3, J)
            norm_row(6, 1, 0, VC[6])
            nbias_row(3, 3)
            norm_row(6, 2, 0, VC[6])
            norm_row(6, 3, VC[6], HALF)
            norm_row(6, 3, 0, VC[6])
            norm_tile(7)
            for j in range(J):
                norm_row(7, j, 0, HALF)

        smh = keep.tile([P, 2], F32, name="smh")
        for h in range(2):
            junk = junkp.tile([P, NPIX], BF16, name="junk")
            nc.scalar.activation(out=junk[:, 0:HALF], in_=x_t[0][:, 0, h * HALF:(h + 1) * HALF], func=ACT.Identity,
                                 scale=1.0 / NPIX, accum_out=smh[:, h:h + 1])
        product_tile(0)
        bn(0, 1, 0)
        bn(0, 1, 1)
        bn(0, 2, 0)
        aggregate(0, 1)
        rstd_vector(0, 1, 2)
        centre_gpsimd(0, 1)
        nc.scalar.activation(out=mu0[:], in_=smh[:, 0:1], func=ACT.Identity, bias=smh[:, 1:2])
        centre_gpsimd(0, 0)
        junk = junkp.tile([P, NPIX], BF16, name="junk")
        nc.scalar.activation(out=junk[:], in_=x_t[0][:, 0, :], func=ACT.Square, scale=-1.0, bias=mu0[:, 0:1],
                             accum_out=ssq[0][:, 0:1])
        bn(0, 2, 1)
        bn(0, 3, 0)
        aggregate(0, 2)
        rstd_vector(0, 2, 3)
        bn(0, 3, 1)
        stage_std_rows(0, STAGED0)
        product0_vector(0, 1)
        nc.vector.memset(minus_t[:], -1.0)
        aggregate(0, 3)
        rstd_scalar(0, 0, 1)
        centre_scalar(0, 2)
        rstd_vector(0, 3, 4)
        centre_scalar(0, 3)
        centre_gpsimd(1, 1)
        centre_gpsimd(1, 0)
        product0_vector(0, 0)
        product0_vector(0, 2)
        product0_vector(0, 3, 0, HALF // 2)
        product0_vector(0, 3, HALF // 2, HALF)
        minus_norm(1, [2, 3])
        add_regroup(0, 0, HALF // 2)
        add_regroup(0, HALF // 2, HALF)
        product_tile(1)
        product_gpsimd(1, 2, J, 0)
        bn(1, 2, 0)
        bn(1, 2, 1)
        bn(1, 3, 0)
        aggregate(1, 2)
        bn(1, 3, 1)
        product0_vector(1, 0)
        aggregate(1, 3)
        product0_vector(1, 1)
        scalar_image1()

        quantise(0)
        weights_quantise()
        multiply(0)
        stage_std(2)
        add_regroup(1)
        for n in range(2, UNITS):
            m = n - 1
            o = n - 2
            if n == 4:
                scalar_image2(False)
            if n == 6:
                scalar_image3()
            product_gpsimd_unit(n)
            if n == 3:
                scalar_image2(True)
            exit_rest(o)
            if n == 2:
                bn(2, 3, 0)
            product_vector(n)
            if n == 3:
                aggregate(2, 3)
            quantise(m)
            multiply(m)
            if n + 1 < UNITS:
                stage_std(n + 1)
            add_regroup(n)

        exit_part(6, 0, 0, HALF, True)
        exit_part(6, 1, 0, HALF, True)
        quantise(7)
        multiply(7)
        exit_part(6, 2, 0, HALF, True)
        exit_part(6, 3, 0, HALF, True)
        for j in range(J - 1):
            exit_part(7, j, 0, HALF, True)
        exit_part(7, J - 1, 0, HALF // 2, True)
        exit_part(7, J - 1, HALF // 2, HALF, True)
